import numpy as np
import ml_dtypes


def mxq(x, axis, fmt="e4m3"):
    dtype, down = {"e4m3": (ml_dtypes.float8_e4m3fn, 7), "e5m2": (ml_dtypes.float8_e5m2, 14)}[fmt]
    v = np.moveaxis(np.asarray(x, np.float32).astype(ml_dtypes.bfloat16).astype(np.float64), axis, -1)
    blocks = v.reshape(v.shape[:-1] + (-1, 32))
    amax = np.abs(blocks).max(-1, keepdims=True)
    byte = np.maximum(np.where(amax > 0, np.frexp(amax)[1] - 1 + 127, 0) - down, 1)
    scale = np.exp2(byte - 127.0)
    codes = (blocks / scale).astype(np.float32).astype(dtype).astype(np.float64)
    return np.moveaxis((codes * scale).reshape(v.shape), -1, axis)


WIDE = False


def mx_kscale(k):
    if not WIDE:
        return np.ones(k)
    levels = np.array([10, -10, 5, -5, 0])
    a = np.random.permutation(np.resize(levels, k // 512 * 4)).reshape(k // 512, 4)
    idx = np.arange(k)
    return np.exp2(a[idx // 512, idx % 128 // 32])


BF16 = ml_dtypes.bfloat16


def bf(x):
    return np.asarray(x, np.float32).astype(BF16)


def f64(x):
    return np.asarray(x).astype(np.float64)


NX, NTEST, DX, DY = 2048, 1024, 256, 256
L_MEAN = 8.0
DM = DX + DY
SIG = 2.0 * L_MEAN / np.sqrt(DM)
ZS = np.exp(4.0) / np.sqrt(NX)


def setup_inputs():
    s = mx_kscale(NX)
    return {"x_mu": bf(np.random.standard_normal((NTEST, DX)) * SIG),
            "y_mean": bf(np.random.standard_normal((NTEST, DY)) * SIG),
            "y_var": bf(np.random.standard_normal((NTEST, DY)) * 0.5 * SIG),
            "X_mean": bf(np.random.standard_normal((NX, DM)) * SIG),
            "Z_mean": bf(np.random.standard_normal((NX, DY)) * ZS / s[:, None]),
            "kXXmean_inv": bf(np.random.standard_normal((NX, NX)) / np.sqrt(NX) * s)}


def reference(x_mu, y_mean, y_var, X_mean, Z_mean, kXXmean_inv):
    X = f64(X_mean)
    x_mean = np.concatenate([f64(x_mu), f64(y_mean) + f64(y_var)], axis=1)
    lam = mxq(f64(kXXmean_inv), 1, "e4m3") @ mxq(f64(Z_mean), 0, "e4m3")
    cross = mxq(X, 1, "e4m3") @ mxq(x_mean, 1, "e4m3").T
    d2 = np.sum(X * X, axis=1)[:, None] + np.sum(x_mean * x_mean, axis=1)[None, :] - 2.0 * cross
    k = np.exp(-np.maximum(d2, 0.0) / (2.0 * L_MEAN * L_MEAN))
    z_mean = mxq(k, 0, "e4m3").T @ mxq(lam, 0, "e4m3")
    return f64(y_mean) + z_mean

@@ -1,0 +1,259 @@
+from contextlib import ExitStack
+
+import concourse.mybir as mybir
+from concourse.masks import make_identity
+
+F32 = mybir.dt.float32
+BF16 = mybir.dt.bfloat16
+U32 = mybir.dt.uint32
+U8 = mybir.dt.uint8
+FP8X4 = mybir.dt.float8_e4m3fn_x4
+ALU = mybir.AluOpType
+ACT = mybir.ActivationFunctionType
+
+P = 128
+PACK = 4
+K_PASS = P * PACK
+
+NX, NT, DX, DY = 2048, 1024, 256, 256
+DM = DX + DY
+GROUPS = NX // K_PASS
+ROW_TILES = NX // P
+Q_TILES = NT // P
+HALF = 512
+KINV_AHEAD = 4
+
+FLOPS = 2 * NX * NX * DY + 2 * NX * NT * DM + 2 * NX * NT * DY
+
+
+def flip_two_blocks(nc, psum, ident, blocks, grouped_words, copy):
+    bank = psum.tile([P, 2, 2, P], F32, tag="flip", bufs=3)
+    for b in range(2):
+        for u in range(2):
+            nc.tensor.transpose(bank[:, b, u, :], blocks[b][:, u * P : (u + 1) * P], ident)
+    copy(out=grouped_words, in_=bank[:].rearrange("q b u r -> q b r u"))
+
+
+def tile_condtransportkernel_pa_kernel(tc, x_mu, y_mean, y_var, X_mean, Z_mean, kXXmean_inv, out):
+    nc = tc.nc
+    with ExitStack() as ctx:
+        keep = ctx.enter_context(tc.tile_pool(name="keep", bufs=1))
+        prep = ctx.enter_context(tc.tile_pool(name="prep", bufs=1))
+        work = ctx.enter_context(tc.tile_pool(name="work", bufs=2))
+        psum = ctx.enter_context(tc.psum_pool(name="psum", bufs=1))
+
+        x_mu_sb = prep.tile([P, Q_TILES, DX], BF16)
+        y_mean_sb = keep.tile([P, Q_TILES, DY], BF16)
+        y_var_sb = prep.tile([P, Q_TILES, DY], BF16)
+        nc.sync.dma_start(out=x_mu_sb[:], in_=x_mu.rearrange("(p a) c -> p a c", a=Q_TILES))
+        nc.sync.dma_start(out=y_mean_sb[:], in_=y_mean.rearrange("(p a) c -> p a c", a=Q_TILES))
+        nc.sync.dma_start(out=y_var_sb[:], in_=y_var.rearrange("(p a) c -> p a c", a=Q_TILES))
+        x_raw = prep.tile([P, GROUPS, PACK, DM], BF16)
+        x_view = X_mean.rearrange("(g p t) c -> g p t c", g=GROUPS, t=PACK)
+        for g in range(GROUPS):
+            nc.sync.dma_start(out=x_raw[:, g], in_=x_view[g])
+        z_raw = prep.tile([P, 2 * GROUPS, 2, DY], BF16)
+        nc.sync.dma_start(out=z_raw[:], in_=Z_mean.rearrange("(s q e) c -> q s e c", q=P, e=2))
+        kinv_view = kXXmean_inv.rearrange("(g p h s) m -> g h p s m", g=GROUPS, h=2, s=2)
+        kinv_raw = []
+
+        def load_kinv(chunk):
+            raw = work.tile([P, 2, NX], BF16, tag="kinv_raw", bufs=KINV_AHEAD, name="kinv_raw")
+            nc.sync.dma_start(out=raw[:], in_=kinv_view[chunk // 2, chunk % 2])
+            kinv_raw.append(raw)
+
+        for chunk in range(KINV_AHEAD):
+            load_kinv(chunk)
+
+        ident = keep.tile([P, P], F32)
+        make_identity(nc, ident[:])
+        zero = keep.tile([P, 1], F32)
+        one = keep.tile([P, 1], F32)
+        nc.vector.memset(zero[:], 0.0)
+        nc.scalar.activation(out=one[:], in_=zero[:], func=ACT.Exp)
+
+        xm32 = prep.tile([P, Q_TILES, PACK, P], F32)
+        yy = keep.tile([P, Q_TILES], F32)
+        square = prep.tile([P, DM], BF16)
+        q_grouped = prep.tile([P, NT, PACK], BF16, align_bytes=64)
+        q_codes = keep.tile([P, NT], U32, align_bytes=64)
+        q_scales = keep.tile([P, NT], U8, align_bytes=64)
+        for h in range(2):
+            rows = slice(h * Q_TILES // 2, (h + 1) * Q_TILES // 2)
+            nc.vector.tensor_copy(
+                out=xm32[:, rows, 0:2, :], in_=x_mu_sb[:, rows, :].rearrange("p a (q e) -> p a e q", e=2)
+            )
+            nc.vector.tensor_tensor(
+                out=xm32[:, rows, 2:4, :],
+                in0=y_mean_sb[:, rows, :].rearrange("p a (q e) -> p a e q", e=2),
+                in1=y_var_sb[:, rows, :].rearrange("p a (q e) -> p a e q", e=2),
+                op=ALU.add,
+            )
+        for a in range(Q_TILES):
+            nc.scalar.activation(
+                out=square[:],
+                in_=xm32[:, a].rearrange("p t q -> p (t q)"),
+                func=ACT.Square,
+                accum_out=yy[:, a : a + 1],
+            )
+        for a in range(Q_TILES):
+            bank = psum.tile([P, PACK, P], F32, tag="flip", bufs=3)
+            for t in range(PACK):
+                nc.tensor.transpose(bank[:, t, :], xm32[:, a, t, :], ident[:])
+            nc.vector.tensor_copy(out=q_grouped[:, a * P : (a + 1) * P, :], in_=bank[:].rearrange("q t j -> q j t"))
+        for h in range(2):
+            cols = slice(h * HALF, (h + 1) * HALF)
+            nc.vector.quantize_mx(
+                out=q_codes[:, cols].bitcast(FP8X4),
+                scales=q_scales[:, cols],
+                in_=q_grouped[:, cols, :].rearrange("q j t -> q (j t)"),
+            )
+
+        yy_rep = prep.tile([P, Q_TILES, P], F32)
+        yy_rows = keep.tile([P, NT], F32)
+        nc.vector.tensor_scalar_mul(
+            out=yy_rep[:], in0=yy[:].unsqueeze(2).to_broadcast([P, Q_TILES, P]), scalar1=0.5
+        )
+        for h in range(2):
+            bank = psum.tile([P, PACK, P], F32, tag="flip", bufs=3)
+            for s in range(PACK):
+                nc.tensor.transpose(bank[:, s, :], yy_rep[:, PACK * h + s, :], ident[:])
+            nc.vector.tensor_copy(out=yy_rows[:, h * HALF : (h + 1) * HALF], in_=bank[:].rearrange("p s j -> p (s j)"))
+
+        x_codes = keep.tile([P, NX], U32, align_bytes=64)
+        x_scales = keep.tile([P, NX], U8, align_bytes=64)
+        xx = keep.tile([P, ROW_TILES], F32)
+        xx_half = keep.tile([P, ROW_TILES], F32)
+        for g in range(GROUPS):
+            x_grouped = prep.tile([P, K_PASS * PACK], BF16, bufs=2, align_bytes=64)
+            x_words = x_grouped[:].bitcast(F32).rearrange("q (t r u) -> q t r u", t=PACK, u=2)
+            for b in range(2):
+                blocks = [x_raw[:, g, 2 * b + s, :].bitcast(F32) for s in range(2)]
+                flip_two_blocks(nc, psum, ident[:], blocks, x_words[:, 2 * b : 2 * b + 2], nc.scalar.copy)
+            cols = slice(g * K_PASS, (g + 1) * K_PASS)
+            nc.vector.quantize_mx(out=x_codes[:, cols].bitcast(FP8X4), scales=x_scales[:, cols], in_=x_grouped[:])
+            for t in range(PACK):
+                nc.scalar.activation(
+                    out=square[:],
+                    in_=x_raw[:, g, t, :],
+                    func=ACT.Square,
+                    accum_out=xx[:, PACK * g + t : PACK * g + t + 1],
+                )
+        nc.vector.tensor_scalar_mul(out=xx_half[:], in0=xx[:], scalar1=0.5)
+
+        z_grouped = prep.tile([P, GROUPS, DY, PACK], BF16, align_bytes=64)
+        z_codes = keep.tile([P, GROUPS, DY], U32, align_bytes=64)
+        z_scales = keep.tile([P, GROUPS, DY], U8, align_bytes=64)
+        z_rows = z_raw[:].rearrange("q (g u) e c -> q g (u e) c", u=2)
+        for g in range(GROUPS):
+            nc.vector.tensor_copy(
+                out=z_grouped[:, g].rearrange("q (c i) t -> q c t i", i=4),
+                in_=z_rows[:, g].rearrange("q t (c i) -> q c t i", i=4),
+            )
+        nc.vector.quantize_mx(
+            out=z_codes[:].rearrange("q g c -> q (g c)").bitcast(FP8X4),
+            scales=z_scales[:].rearrange("q g c -> q (g c)"),
+            in_=z_grouped[:].rearrange("q g c t -> q (g c t)"),
+        )
+
+        lam_codes = keep.tile([P, GROUPS, DY], U32, align_bytes=64)
+        lam_scales = keep.tile([P, GROUPS, DY], U8, align_bytes=64)
+        k_codes = keep.tile([P, 2 * GROUPS, HALF], U32, align_bytes=64)
+        k_scales = keep.tile([P, 2 * GROUPS, HALF], U8, align_bytes=64)
+        lam_banks = []
+        for step in range(2 * GROUPS):
+            if step % 2 == 0:
+                lam_lo = psum.tile([P, PACK, P], F32)
+                lam_hi = psum.tile([P, PACK, P], F32)
+                lam_banks = [lam_lo, lam_hi]
+            for s in range(2):
+                t = 2 * (step % 2) + s
+                words = kinv_raw[step][:, s, :].bitcast(F32)
+                kinv_grouped = work.tile([P, NX], BF16, bufs=3, align_bytes=64)
+                kinv_words = kinv_grouped[:].bitcast(F32).rearrange("q (g r u) -> q g r u", g=GROUPS, u=2)
+                for b in range(2):
+                    blocks = [words[:, (2 * b + c) * 2 * P : (2 * b + c + 1) * 2 * P] for c in range(2)]
+                    flip_two_blocks(nc, psum, ident[:], blocks, kinv_words[:, 2 * b : 2 * b + 2], nc.scalar.copy)
+                kinv_codes = work.tile([P, GROUPS * P], U32, bufs=3, align_bytes=64)
+                kinv_scales = work.tile([P, GROUPS * P], U8, bufs=3, align_bytes=64)
+                nc.vector.quantize_mx(out=kinv_codes[:].bitcast(FP8X4), scales=kinv_scales[:], in_=kinv_grouped[:])
+                for dh in range(2):
+                    for g in range(GROUPS):
+                        nc.tensor.matmul_mx(
+                            out=lam_banks[dh][:, t, :],
+                            lhsT=kinv_codes[:, g * P : (g + 1) * P].bitcast(FP8X4),
+                            lhsT_scale=kinv_scales[:, g * P : (g + 1) * P],
+                            rhs=z_codes[:, g, dh * P : (dh + 1) * P].bitcast(FP8X4),
+                            rhs_scale=z_scales[:, g, dh * P : (dh + 1) * P],
+                            start=(g == 0),
+                            stop=(g == GROUPS - 1),
+                        )
+            if step + KINV_AHEAD < 2 * GROUPS:
+                load_kinv(step + KINV_AHEAD)
+            if step % 2 == 1:
+                lam_group = step // 2
+                lam_grouped = work.tile([P, DY, PACK], BF16, align_bytes=64)
+                for dh in range(2):
+                    nc.scalar.copy(
+                        out=lam_grouped[:, dh * P : (dh + 1) * P, :], in_=lam_banks[dh][:].rearrange("p t d -> p d t")
+                    )
+                nc.vector.quantize_mx(
+                    out=lam_codes[:, lam_group, :].bitcast(FP8X4),
+                    scales=lam_scales[:, lam_group, :],
+                    in_=lam_grouped[:].rearrange("p d t -> p (d t)"),
+                )
+
+            half, group = divmod(step, GROUPS)
+            cols = slice(half * HALF, (half + 1) * HALF)
+            minus_half_d2 = work.tile([P, PACK, HALF], F32)
+            for t in range(PACK):
+                tile_no = PACK * group + t
+                cross = psum.tile([P, HALF], F32, tag="cross", bufs=3)
+                nc.tensor.matmul_mx(
+                    out=cross[:],
+                    lhsT=x_codes[:, tile_no * P : (tile_no + 1) * P].bitcast(FP8X4),
+                    lhsT_scale=x_scales[:, tile_no * P : (tile_no + 1) * P],
+                    rhs=q_codes[:, cols].bitcast(FP8X4),
+                    rhs_scale=q_scales[:, cols],
+                    start=True,
+                    stop=True,
+                )
+                nc.vector.scalar_tensor_tensor(
+                    out=minus_half_d2[:, t, :],
+                    in0=cross[:],
+                    scalar=xx_half[:, tile_no : tile_no + 1],
+                    in1=yy_rows[:, cols],
+                    op0=ALU.subtract,
+                    op1=ALU.subtract,
+                )
+            k_grouped = work.tile([P, HALF, PACK], BF16, align_bytes=64)
+            nc.scalar.activation(
+                out=k_grouped[:].rearrange("p (c i) t -> p c t i", i=4),
+                in_=minus_half_d2[:].rearrange("p t (c i) -> p c t i", i=4),
+                func=ACT.Exp,
+                scale=1.0 / 64.0,
+            )
+            k_flat = k_grouped[:].rearrange("p j t -> p (j t)")
+            nc.vector.tensor_scalar_min(out=k_flat, in0=k_flat, scalar1=1.0)
+            nc.vector.quantize_mx(out=k_codes[:, step, :].bitcast(FP8X4), scales=k_scales[:, step, :], in_=k_flat)
+
+        out_view = out.rearrange("(p a) d -> p a d", a=Q_TILES)
+        for pair in range(Q_TILES // 2):
+            acc = psum.tile([P, 2, DY], F32, tag="cross", bufs=3)
+            for s in range(2):
+                half, col = divmod(2 * pair + s, Q_TILES // 2)
+                for g in range(GROUPS):
+                    nc.tensor.matmul_mx(
+                        out=acc[:, s, :],
+                        lhsT=k_codes[:, GROUPS * half + g, col * P : (col + 1) * P].bitcast(FP8X4),
+                        lhsT_scale=k_scales[:, GROUPS * half + g, col * P : (col + 1) * P],
+                        rhs=lam_codes[:, g, :].bitcast(FP8X4),
+                        rhs_scale=lam_scales[:, g, :],
+                        start=(g == 0),
+                        stop=(g == GROUPS - 1),
+                    )
+            result = work.tile([P, 2, DY], F32)
+            nc.vector.tensor_tensor(
+                out=result[:], in0=acc[:], in1=y_mean_sb[:, 2 * pair : 2 * pair + 2, :], op=ALU.add
+            )
+            nc.sync.dma_start(out=out_view[:, 2 * pair : 2 * pair + 2, :], in_=result[:])

@@ -18,201 +18,192 @@ K_PASS = P * PACK
 NX, NT, DX, DY = 2048, 1024, 256, 256
 DM = DX + DY
 GROUPS = NX // K_PASS
-ROW_TILES = NX // P
 Q_TILES = NT // P
 HALF = 512
+HALF_TILES = HALF // P
+STEPS = 2 * GROUPS
 KINV_AHEAD = 4
 
 FLOPS = 2 * NX * NX * DY + 2 * NX * NT * DM + 2 * NX * NT * DY
-
-
-def flip_two_blocks(nc, psum, ident, blocks, grouped_words, copy):
-    bank = psum.tile([P, 2, 2, P], F32, tag="flip", bufs=3)
-    for b in range(2):
-        for u in range(2):
-            nc.tensor.transpose(bank[:, b, u, :], blocks[b][:, u * P : (u + 1) * P], ident)
-    copy(out=grouped_words, in_=bank[:].rearrange("q b u r -> q b r u"))
 
 
 def tile_condtransportkernel_pa_kernel(tc, x_mu, y_mean, y_var, X_mean, Z_mean, kXXmean_inv, out):
     nc = tc.nc
     with ExitStack() as ctx:
         keep = ctx.enter_context(tc.tile_pool(name="keep", bufs=1))
-        prep = ctx.enter_context(tc.tile_pool(name="prep", bufs=1))
         work = ctx.enter_context(tc.tile_pool(name="work", bufs=2))
         psum = ctx.enter_context(tc.psum_pool(name="psum", bufs=1))
 
-        x_mu_sb = prep.tile([P, Q_TILES, DX], BF16)
+        x_mu_sb = keep.tile([P, Q_TILES, DX], BF16)
         y_mean_sb = keep.tile([P, Q_TILES, DY], BF16)
-        y_var_sb = prep.tile([P, Q_TILES, DY], BF16)
-        nc.sync.dma_start(out=x_mu_sb[:], in_=x_mu.rearrange("(p a) c -> p a c", a=Q_TILES))
-        nc.sync.dma_start(out=y_mean_sb[:], in_=y_mean.rearrange("(p a) c -> p a c", a=Q_TILES))
-        nc.sync.dma_start(out=y_var_sb[:], in_=y_var.rearrange("(p a) c -> p a c", a=Q_TILES))
-        x_raw = prep.tile([P, GROUPS, PACK, DM], BF16)
-        x_view = X_mean.rearrange("(g p t) c -> g p t c", g=GROUPS, t=PACK)
-        for g in range(GROUPS):
-            nc.sync.dma_start(out=x_raw[:, g], in_=x_view[g])
-        z_raw = prep.tile([P, 2 * GROUPS, 2, DY], BF16)
-        nc.sync.dma_start(out=z_raw[:], in_=Z_mean.rearrange("(s q e) c -> q s e c", q=P, e=2))
-        kinv_view = kXXmean_inv.rearrange("(g p h s) m -> g h p s m", g=GROUPS, h=2, s=2)
+        y_var_sb = keep.tile([P, Q_TILES, DY], BF16)
+        x_raw = keep.tile([P, GROUPS, PACK, DM], BF16)
+        z_raw = keep.tile([P, 2 * GROUPS, 2, DY], BF16)
+        ident = keep.tile([P, P], F32)
+        q_codes = keep.tile([P, NT], U32, align_bytes=64)
+        q_scales = keep.tile([P, NT], U8, align_bytes=64)
+        yy = keep.tile([P, Q_TILES], F32)
+        yy_rows = keep.tile([P, NT], F32)
+        x_codes = keep.tile([P, NX], U32, align_bytes=64)
+        x_scales = keep.tile([P, NX], U8, align_bytes=64)
+        xx = keep.tile([P, GROUPS, PACK], F32)
+        xx_half = keep.tile([P, GROUPS, PACK], F32)
+        z_codes = keep.tile([P, GROUPS, DY], U32, align_bytes=64)
+        z_scales = keep.tile([P, GROUPS, DY], U8, align_bytes=64)
+        lam_codes = keep.tile([P, GROUPS, DY], U32, align_bytes=64)
+        lam_scales = keep.tile([P, GROUPS, DY], U8, align_bytes=64)
+        k_codes = keep.tile([P, STEPS, HALF], U32, align_bytes=64)
+        k_scales = keep.tile([P, STEPS, HALF], U8, align_bytes=64)
         kinv_raw = []
+
+        def load_queries(half):
+            rows = slice(half * HALF_TILES, (half + 1) * HALF_TILES)
+            for sb, dram in ((x_mu_sb, x_mu), (y_mean_sb, y_mean), (y_var_sb, y_var)):
+                nc.sync.dma_start(out=sb[:, rows, :], in_=dram.rearrange("(p a) c -> p a c", a=Q_TILES)[:, rows, :])
+
+        def load_points(g):
+            nc.sync.dma_start(out=x_raw[:, g], in_=X_mean.rearrange("(g p t) c -> g p t c", g=GROUPS, t=PACK)[g])
 
         def load_kinv(chunk):
             raw = work.tile([P, 2, NX], BF16, tag="kinv_raw", bufs=KINV_AHEAD, name="kinv_raw")
-            nc.sync.dma_start(out=raw[:], in_=kinv_view[chunk // 2, chunk % 2])
+            view = kXXmean_inv.rearrange("(g p h s) m -> g h p s m", g=GROUPS, h=2, s=2)
+            nc.sync.dma_start(out=raw[:], in_=view[chunk // 2, chunk % 2])
             kinv_raw.append(raw)
 
-        for chunk in range(KINV_AHEAD):
-            load_kinv(chunk)
+        load_queries(0)
+        load_points(0)
+        nc.sync.dma_start(out=z_raw[:], in_=Z_mean.rearrange("(s q e) c -> q s e c", q=P, e=2))
+        load_kinv(0)
+        load_queries(1)
+        for g in range(1, GROUPS):
+            load_points(g)
+            load_kinv(g)
 
-        ident = keep.tile([P, P], F32)
         make_identity(nc, ident[:])
         zero = keep.tile([P, 1], F32)
         one = keep.tile([P, 1], F32)
         nc.vector.memset(zero[:], 0.0)
         nc.scalar.activation(out=one[:], in_=zero[:], func=ACT.Exp)
 
-        xm32 = prep.tile([P, Q_TILES, PACK, P], F32)
-        yy = keep.tile([P, Q_TILES], F32)
-        square = prep.tile([P, DM], BF16)
-        q_grouped = prep.tile([P, NT, PACK], BF16, align_bytes=64)
-        q_codes = keep.tile([P, NT], U32, align_bytes=64)
-        q_scales = keep.tile([P, NT], U8, align_bytes=64)
-        for h in range(2):
-            rows = slice(h * Q_TILES // 2, (h + 1) * Q_TILES // 2)
-            nc.vector.tensor_copy(
-                out=xm32[:, rows, 0:2, :], in_=x_mu_sb[:, rows, :].rearrange("p a (q e) -> p a e q", e=2)
-            )
+        def flip_two_blocks(blocks, grouped_words, copy):
+            bank = psum.tile([P, 2, 2, P], F32, tag="flip", bufs=3)
+            for b in range(2):
+                for u in range(2):
+                    nc.tensor.transpose(bank[:, b, u, :], blocks[b][:, u * P : (u + 1) * P], ident[:])
+            copy(out=grouped_words, in_=bank[:].rearrange("q b u r -> q b r u"))
+
+        def prepare_queries(half):
+            rows = slice(half * HALF_TILES, (half + 1) * HALF_TILES)
+            cols = slice(half * HALF, (half + 1) * HALF)
+            xm32 = work.tile([P, HALF_TILES, PACK, P], F32, bufs=1)
+            nc.scalar.copy(out=xm32[:, :, 0:2, :], in_=x_mu_sb[:, rows, :].rearrange("p a (q e) -> p a e q", e=2))
             nc.vector.tensor_tensor(
-                out=xm32[:, rows, 2:4, :],
+                out=xm32[:, :, 2:4, :],
                 in0=y_mean_sb[:, rows, :].rearrange("p a (q e) -> p a e q", e=2),
                 in1=y_var_sb[:, rows, :].rearrange("p a (q e) -> p a e q", e=2),
                 op=ALU.add,
             )
-        for a in range(Q_TILES):
-            nc.scalar.activation(
-                out=square[:],
-                in_=xm32[:, a].rearrange("p t q -> p (t q)"),
-                func=ACT.Square,
-                accum_out=yy[:, a : a + 1],
-            )
-        for a in range(Q_TILES):
-            bank = psum.tile([P, PACK, P], F32, tag="flip", bufs=3)
-            for t in range(PACK):
-                nc.tensor.transpose(bank[:, t, :], xm32[:, a, t, :], ident[:])
-            nc.vector.tensor_copy(out=q_grouped[:, a * P : (a + 1) * P, :], in_=bank[:].rearrange("q t j -> q j t"))
-        for h in range(2):
-            cols = slice(h * HALF, (h + 1) * HALF)
+            q_grouped = work.tile([P, HALF, PACK], BF16, bufs=1, align_bytes=64)
+            for a in range(HALF_TILES):
+                square = work.tile([P, DM], BF16, tag="square")
+                nc.scalar.activation(
+                    out=square[:],
+                    in_=xm32[:, a].rearrange("p t q -> p (t q)"),
+                    func=ACT.Square,
+                    accum_out=yy[:, half * HALF_TILES + a : half * HALF_TILES + a + 1],
+                )
+                bank = psum.tile([P, PACK, P], F32, tag="flip", bufs=3)
+                for t in range(PACK):
+                    nc.tensor.transpose(bank[:, t, :], xm32[:, a, t, :], ident[:])
+                nc.vector.tensor_copy(
+                    out=q_grouped[:, a * P : (a + 1) * P, :], in_=bank[:].rearrange("q t j -> q j t")
+                )
             nc.vector.quantize_mx(
                 out=q_codes[:, cols].bitcast(FP8X4),
                 scales=q_scales[:, cols],
-                in_=q_grouped[:, cols, :].rearrange("q j t -> q (j t)"),
+                in_=q_grouped[:].rearrange("q j t -> q (j t)"),
             )
+            yy_rep = work.tile([P, HALF_TILES, P], F32, bufs=1)
+            nc.vector.tensor_scalar_mul(
+                out=yy_rep[:], in0=yy[:, rows].unsqueeze(2).to_broadcast([P, HALF_TILES, P]), scalar1=0.5
+            )
+            bank = psum.tile([P, HALF_TILES, P], F32, tag="flip", bufs=3)
+            for a in range(HALF_TILES):
+                nc.tensor.transpose(bank[:, a, :], yy_rep[:, a, :], ident[:])
+            nc.vector.tensor_copy(out=yy_rows[:, cols], in_=bank[:].rearrange("p a j -> p (a j)"))
 
-        yy_rep = prep.tile([P, Q_TILES, P], F32)
-        yy_rows = keep.tile([P, NT], F32)
-        nc.vector.tensor_scalar_mul(
-            out=yy_rep[:], in0=yy[:].unsqueeze(2).to_broadcast([P, Q_TILES, P]), scalar1=0.5
-        )
-        for h in range(2):
-            bank = psum.tile([P, PACK, P], F32, tag="flip", bufs=3)
-            for s in range(PACK):
-                nc.tensor.transpose(bank[:, s, :], yy_rep[:, PACK * h + s, :], ident[:])
-            nc.vector.tensor_copy(out=yy_rows[:, h * HALF : (h + 1) * HALF], in_=bank[:].rearrange("p s j -> p (s j)"))
-
-        x_codes = keep.tile([P, NX], U32, align_bytes=64)
-        x_scales = keep.tile([P, NX], U8, align_bytes=64)
-        xx = keep.tile([P, ROW_TILES], F32)
-        xx_half = keep.tile([P, ROW_TILES], F32)
-        for g in range(GROUPS):
-            x_grouped = prep.tile([P, K_PASS * PACK], BF16, bufs=2, align_bytes=64)
+        def prepare_points(g):
+            x_grouped = work.tile([P, K_PASS * PACK], BF16, align_bytes=64)
             x_words = x_grouped[:].bitcast(F32).rearrange("q (t r u) -> q t r u", t=PACK, u=2)
             for b in range(2):
                 blocks = [x_raw[:, g, 2 * b + s, :].bitcast(F32) for s in range(2)]
-                flip_two_blocks(nc, psum, ident[:], blocks, x_words[:, 2 * b : 2 * b + 2], nc.scalar.copy)
+                flip_two_blocks(blocks, x_words[:, 2 * b : 2 * b + 2], nc.scalar.copy)
             cols = slice(g * K_PASS, (g + 1) * K_PASS)
             nc.vector.quantize_mx(out=x_codes[:, cols].bitcast(FP8X4), scales=x_scales[:, cols], in_=x_grouped[:])
             for t in range(PACK):
+                square = work.tile([P, DM], BF16, tag="square")
                 nc.scalar.activation(
-                    out=square[:],
-                    in_=x_raw[:, g, t, :],
-                    func=ACT.Square,
-                    accum_out=xx[:, PACK * g + t : PACK * g + t + 1],
+                    out=square[:], in_=x_raw[:, g, t, :], func=ACT.Square, accum_out=xx[:, g, t : t + 1]
                 )
-        nc.vector.tensor_scalar_mul(out=xx_half[:], in0=xx[:], scalar1=0.5)
+            nc.vector.tensor_scalar_mul(out=xx_half[:, g, :], in0=xx[:, g, :], scalar1=0.5)
 
-        z_grouped = prep.tile([P, GROUPS, DY, PACK], BF16, align_bytes=64)
-        z_codes = keep.tile([P, GROUPS, DY], U32, align_bytes=64)
-        z_scales = keep.tile([P, GROUPS, DY], U8, align_bytes=64)
-        z_rows = z_raw[:].rearrange("q (g u) e c -> q g (u e) c", u=2)
-        for g in range(GROUPS):
-            nc.vector.tensor_copy(
-                out=z_grouped[:, g].rearrange("q (c i) t -> q c t i", i=4),
-                in_=z_rows[:, g].rearrange("q t (c i) -> q c t i", i=4),
+        def prepare_z():
+            z_grouped = work.tile([P, GROUPS, DY, PACK], BF16, bufs=1, align_bytes=64)
+            z_rows = z_raw[:].rearrange("q (g u) e c -> q g (u e) c", u=2)
+            for g in range(GROUPS):
+                nc.vector.tensor_copy(
+                    out=z_grouped[:, g].rearrange("q (c i) t -> q c t i", i=4),
+                    in_=z_rows[:, g].rearrange("q t (c i) -> q c t i", i=4),
+                )
+            nc.vector.quantize_mx(
+                out=z_codes[:].rearrange("q g c -> q (g c)").bitcast(FP8X4),
+                scales=z_scales[:].rearrange("q g c -> q (g c)"),
+                in_=z_grouped[:].rearrange("q g c t -> q (g c t)"),
             )
-        nc.vector.quantize_mx(
-            out=z_codes[:].rearrange("q g c -> q (g c)").bitcast(FP8X4),
-            scales=z_scales[:].rearrange("q g c -> q (g c)"),
-            in_=z_grouped[:].rearrange("q g c t -> q (g c t)"),
-        )
 
-        lam_codes = keep.tile([P, GROUPS, DY], U32, align_bytes=64)
-        lam_scales = keep.tile([P, GROUPS, DY], U8, align_bytes=64)
-        k_codes = keep.tile([P, 2 * GROUPS, HALF], U32, align_bytes=64)
-        k_scales = keep.tile([P, 2 * GROUPS, HALF], U8, align_bytes=64)
-        lam_banks = []
-        for step in range(2 * GROUPS):
-            if step % 2 == 0:
-                lam_lo = psum.tile([P, PACK, P], F32)
-                lam_hi = psum.tile([P, PACK, P], F32)
-                lam_banks = [lam_lo, lam_hi]
-            for s in range(2):
-                t = 2 * (step % 2) + s
-                words = kinv_raw[step][:, s, :].bitcast(F32)
-                kinv_grouped = work.tile([P, NX], BF16, bufs=3, align_bytes=64)
-                kinv_words = kinv_grouped[:].bitcast(F32).rearrange("q (g r u) -> q g r u", g=GROUPS, u=2)
-                for b in range(2):
-                    blocks = [words[:, (2 * b + c) * 2 * P : (2 * b + c + 1) * 2 * P] for c in range(2)]
-                    flip_two_blocks(nc, psum, ident[:], blocks, kinv_words[:, 2 * b : 2 * b + 2], nc.scalar.copy)
-                kinv_codes = work.tile([P, GROUPS * P], U32, bufs=3, align_bytes=64)
-                kinv_scales = work.tile([P, GROUPS * P], U8, bufs=3, align_bytes=64)
-                nc.vector.quantize_mx(out=kinv_codes[:].bitcast(FP8X4), scales=kinv_scales[:], in_=kinv_grouped[:])
-                for dh in range(2):
-                    for g in range(GROUPS):
-                        nc.tensor.matmul_mx(
-                            out=lam_banks[dh][:, t, :],
-                            lhsT=kinv_codes[:, g * P : (g + 1) * P].bitcast(FP8X4),
-                            lhsT_scale=kinv_scales[:, g * P : (g + 1) * P],
-                            rhs=z_codes[:, g, dh * P : (dh + 1) * P].bitcast(FP8X4),
-                            rhs_scale=z_scales[:, g, dh * P : (dh + 1) * P],
-                            start=(g == 0),
-                            stop=(g == GROUPS - 1),
-                        )
-            if step + KINV_AHEAD < 2 * GROUPS:
-                load_kinv(step + KINV_AHEAD)
-            if step % 2 == 1:
-                lam_group = step // 2
-                lam_grouped = work.tile([P, DY, PACK], BF16, align_bytes=64)
-                for dh in range(2):
-                    nc.scalar.copy(
-                        out=lam_grouped[:, dh * P : (dh + 1) * P, :], in_=lam_banks[dh][:].rearrange("p t d -> p d t")
+        def lam_row_tile(raw_rows, t, lam_banks):
+            words = raw_rows.bitcast(F32)
+            kinv_grouped = work.tile([P, NX], BF16, bufs=3, align_bytes=64)
+            kinv_words = kinv_grouped[:].bitcast(F32).rearrange("q (g r u) -> q g r u", g=GROUPS, u=2)
+            for b in range(2):
+                blocks = [words[:, (2 * b + c) * 2 * P : (2 * b + c + 1) * 2 * P] for c in range(2)]
+                flip_two_blocks(blocks, kinv_words[:, 2 * b : 2 * b + 2], nc.scalar.copy)
+            kinv_codes = work.tile([P, GROUPS * P], U32, bufs=3, align_bytes=64)
+            kinv_scales = work.tile([P, GROUPS * P], U8, bufs=3, align_bytes=64)
+            nc.vector.quantize_mx(out=kinv_codes[:].bitcast(FP8X4), scales=kinv_scales[:], in_=kinv_grouped[:])
+            for dh in range(2):
+                for g in range(GROUPS):
+                    nc.tensor.matmul_mx(
+                        out=lam_banks[dh][:, t, :],
+                        lhsT=kinv_codes[:, g * P : (g + 1) * P].bitcast(FP8X4),
+                        lhsT_scale=kinv_scales[:, g * P : (g + 1) * P],
+                        rhs=z_codes[:, g, dh * P : (dh + 1) * P].bitcast(FP8X4),
+                        rhs_scale=z_scales[:, g, dh * P : (dh + 1) * P],
+                        start=(g == 0),
+                        stop=(g == GROUPS - 1),
                     )
-                nc.vector.quantize_mx(
-                    out=lam_codes[:, lam_group, :].bitcast(FP8X4),
-                    scales=lam_scales[:, lam_group, :],
-                    in_=lam_grouped[:].rearrange("p d t -> p (d t)"),
-                )
 
+        def quantise_lam(group, lam_banks):
+            lam_grouped = work.tile([P, DY, PACK], BF16, align_bytes=64)
+            nc.scalar.copy(out=lam_grouped[:, 0:P, :], in_=lam_banks[0][:].rearrange("p t d -> p d t"))
+            nc.vector.tensor_copy(out=lam_grouped[:, P:DY, :], in_=lam_banks[1][:].rearrange("p t d -> p d t"))
+            nc.vector.quantize_mx(
+                out=lam_codes[:, group, :].bitcast(FP8X4),
+                scales=lam_scales[:, group, :],
+                in_=lam_grouped[:].rearrange("p d t -> p (d t)"),
+            )
+
+        def k_piece(step):
             half, group = divmod(step, GROUPS)
             cols = slice(half * HALF, (half + 1) * HALF)
             minus_half_d2 = work.tile([P, PACK, HALF], F32)
             for t in range(PACK):
-                tile_no = PACK * group + t
+                points = slice((PACK * group + t) * P, (PACK * group + t + 1) * P)
                 cross = psum.tile([P, HALF], F32, tag="cross", bufs=3)
                 nc.tensor.matmul_mx(
                     out=cross[:],
-                    lhsT=x_codes[:, tile_no * P : (tile_no + 1) * P].bitcast(FP8X4),
-                    lhsT_scale=x_scales[:, tile_no * P : (tile_no + 1) * P],
+                    lhsT=x_codes[:, points].bitcast(FP8X4),
+                    lhsT_scale=x_scales[:, points],
                     rhs=q_codes[:, cols].bitcast(FP8X4),
                     rhs_scale=q_scales[:, cols],
                     start=True,
@@ -221,30 +212,34 @@ def tile_condtransportkernel_pa_kernel(tc, x_mu, y_mean, y_var, X_mean, Z_mean, 
                 nc.vector.scalar_tensor_tensor(
                     out=minus_half_d2[:, t, :],
                     in0=cross[:],
-                    scalar=xx_half[:, tile_no : tile_no + 1],
+                    scalar=xx_half[:, group, t : t + 1],
                     in1=yy_rows[:, cols],
                     op0=ALU.subtract,
                     op1=ALU.subtract,
                 )
             k_grouped = work.tile([P, HALF, PACK], BF16, align_bytes=64)
-            nc.scalar.activation(
-                out=k_grouped[:].rearrange("p (c i) t -> p c t i", i=4),
-                in_=minus_half_d2[:].rearrange("p t (c i) -> p c t i", i=4),
-                func=ACT.Exp,
-                scale=1.0 / 64.0,
-            )
-            k_flat = k_grouped[:].rearrange("p j t -> p (j t)")
-            nc.vector.tensor_scalar_min(out=k_flat, in0=k_flat, scalar1=1.0)
-            nc.vector.quantize_mx(out=k_codes[:, step, :].bitcast(FP8X4), scales=k_scales[:, step, :], in_=k_flat)
+            for sub in range(2):
+                queries = slice(sub * HALF // 2, (sub + 1) * HALF // 2)
+                nc.scalar.activation(
+                    out=k_grouped[:, queries, :].rearrange("p (c i) t -> p c t i", i=4),
+                    in_=minus_half_d2[:, :, queries].rearrange("p t (c i) -> p c t i", i=4),
+                    func=ACT.Exp,
+                    scale=1.0 / 64.0,
+                )
+                k_flat = k_grouped[:, queries, :].rearrange("p j t -> p (j t)")
+                nc.vector.tensor_scalar_min(out=k_flat, in0=k_flat, scalar1=1.0)
+                nc.vector.quantize_mx(
+                    out=k_codes[:, step, queries].bitcast(FP8X4), scales=k_scales[:, step, queries], in_=k_flat
+                )
 
-        out_view = out.rearrange("(p a) d -> p a d", a=Q_TILES)
-        for pair in range(Q_TILES // 2):
-            acc = psum.tile([P, 2, DY], F32, tag="cross", bufs=3)
+        def out_pair(pair):
+            result = work.tile([P, 2, DY], F32)
             for s in range(2):
-                half, col = divmod(2 * pair + s, Q_TILES // 2)
+                half, col = divmod(2 * pair + s, HALF_TILES)
+                acc = psum.tile([P, DY], F32, tag="cross", bufs=3)
                 for g in range(GROUPS):
                     nc.tensor.matmul_mx(
-                        out=acc[:, s, :],
+                        out=acc[:],
                         lhsT=k_codes[:, GROUPS * half + g, col * P : (col + 1) * P].bitcast(FP8X4),
                         lhsT_scale=k_scales[:, GROUPS * half + g, col * P : (col + 1) * P],
                         rhs=lam_codes[:, g, :].bitcast(FP8X4),
@@ -252,8 +247,29 @@ def tile_condtransportkernel_pa_kernel(tc, x_mu, y_mean, y_var, X_mean, Z_mean, 
                         start=(g == 0),
                         stop=(g == GROUPS - 1),
                     )
-            result = work.tile([P, 2, DY], F32)
-            nc.vector.tensor_tensor(
-                out=result[:], in0=acc[:], in1=y_mean_sb[:, 2 * pair : 2 * pair + 2, :], op=ALU.add
+                nc.vector.tensor_tensor(out=result[:, s, :], in0=acc[:], in1=y_mean_sb[:, 2 * pair + s, :], op=ALU.add)
+            nc.sync.dma_start(
+                out=out.rearrange("(p a) d -> p a d", a=Q_TILES)[:, 2 * pair : 2 * pair + 2, :], in_=result[:]
             )
-            nc.sync.dma_start(out=out_view[:, 2 * pair : 2 * pair + 2, :], in_=result[:])
+
+        prepare_queries(0)
+        prepare_points(0)
+        prepare_z()
+        for lam_group in range(GROUPS):
+            lam_lo = psum.tile([P, PACK, P], F32)
+            lam_hi = psum.tile([P, PACK, P], F32)
+            for part in range(2):
+                step = 2 * lam_group + part
+                for s in range(2):
+                    lam_row_tile(kinv_raw[step][:, s, :], 2 * part + s, [lam_lo, lam_hi])
+                if step + KINV_AHEAD < STEPS:
+                    load_kinv(step + KINV_AHEAD)
+                if part == 1:
+                    quantise_lam(lam_group, [lam_lo, lam_hi])
+                k_piece(step)
+                if step + 1 < GROUPS:
+                    prepare_points(step + 1)
+                if step == 1:
+                    prepare_queries(1)
+        for pair in range(Q_TILES // 2):
+            out_pair(pair)

@@ -54,7 +54,6 @@ def tile_condtransportkernel_pa_kernel(tc, x_mu, y_mean, y_var, X_mean, Z_mean, 
         lam_scales = keep.tile([P, GROUPS, DY], U8, align_bytes=64)
         k_codes = keep.tile([P, STEPS, HALF], U32, align_bytes=64)
         k_scales = keep.tile([P, STEPS, HALF], U8, align_bytes=64)
-        kinv_raw = []
 
         def load_queries(half):
             rows = slice(half * HALF_TILES, (half + 1) * HALF_TILES)
@@ -64,20 +63,23 @@ def tile_condtransportkernel_pa_kernel(tc, x_mu, y_mean, y_var, X_mean, Z_mean, 
         def load_points(g):
             nc.sync.dma_start(out=x_raw[:, g], in_=X_mean.rearrange("(g p t) c -> g p t c", g=GROUPS, t=PACK)[g])
 
-        def load_kinv(chunk):
+        def load_kinv(step):
             raw = work.tile([P, 2, NX], BF16, tag="kinv_raw", bufs=KINV_AHEAD, name="kinv_raw")
             view = kXXmean_inv.rearrange("(g p h s) m -> g h p s m", g=GROUPS, h=2, s=2)
-            nc.sync.dma_start(out=raw[:], in_=view[chunk // 2, chunk % 2])
-            kinv_raw.append(raw)
+            nc.sync.dma_start(out=raw[:], in_=view[step // 2, step % 2])
+            return raw
 
         load_queries(0)
         load_points(0)
-        nc.sync.dma_start(out=z_raw[:], in_=Z_mean.rearrange("(s q e) c -> q s e c", q=P, e=2))
-        load_kinv(0)
         load_queries(1)
-        for g in range(1, GROUPS):
-            load_points(g)
-            load_kinv(g)
+        load_points(1)
+        nc.sync.dma_start(out=z_raw[:], in_=Z_mean.rearrange("(s q e) c -> q s e c", q=P, e=2))
+        kinv_raw = {0: load_kinv(0)}
+        load_points(2)
+        kinv_raw[1] = load_kinv(1)
+        load_points(3)
+        kinv_raw[2] = load_kinv(2)
+        kinv_raw[3] = load_kinv(3)
 
         make_identity(nc, ident[:])
         zero = keep.tile([P, 1], F32)
@@ -86,7 +88,7 @@ def tile_condtransportkernel_pa_kernel(tc, x_mu, y_mean, y_var, X_mean, Z_mean, 
         nc.scalar.activation(out=one[:], in_=zero[:], func=ACT.Exp)
 
         def flip_two_blocks(blocks, grouped_words, copy):
-            bank = psum.tile([P, 2, 2, P], F32, tag="flip", bufs=3)
+            bank = psum.tile([P, 2, 2, P], F32, tag="bank", bufs=8)
             for b in range(2):
                 for u in range(2):
                     nc.tensor.transpose(bank[:, b, u, :], blocks[b][:, u * P : (u + 1) * P], ident[:])
@@ -95,7 +97,7 @@ def tile_condtransportkernel_pa_kernel(tc, x_mu, y_mean, y_var, X_mean, Z_mean, 
         def prepare_queries(half):
             rows = slice(half * HALF_TILES, (half + 1) * HALF_TILES)
             cols = slice(half * HALF, (half + 1) * HALF)
-            xm32 = work.tile([P, HALF_TILES, PACK, P], F32, bufs=1)
+            xm32 = work.tile([P, HALF_TILES, PACK, P], F32)
             nc.scalar.copy(out=xm32[:, :, 0:2, :], in_=x_mu_sb[:, rows, :].rearrange("p a (q e) -> p a e q", e=2))
             nc.vector.tensor_tensor(
                 out=xm32[:, :, 2:4, :],
@@ -103,7 +105,7 @@ def tile_condtransportkernel_pa_kernel(tc, x_mu, y_mean, y_var, X_mean, Z_mean, 
                 in1=y_var_sb[:, rows, :].rearrange("p a (q e) -> p a e q", e=2),
                 op=ALU.add,
             )
-            q_grouped = work.tile([P, HALF, PACK], BF16, bufs=1, align_bytes=64)
+            q_grouped = work.tile([P, HALF, PACK], BF16, align_bytes=64)
             for a in range(HALF_TILES):
                 square = work.tile([P, DM], BF16, tag="square")
                 nc.scalar.activation(
@@ -112,7 +114,7 @@ def tile_condtransportkernel_pa_kernel(tc, x_mu, y_mean, y_var, X_mean, Z_mean, 
                     func=ACT.Square,
                     accum_out=yy[:, half * HALF_TILES + a : half * HALF_TILES + a + 1],
                 )
-                bank = psum.tile([P, PACK, P], F32, tag="flip", bufs=3)
+                bank = psum.tile([P, PACK, P], F32, tag="bank", bufs=8)
                 for t in range(PACK):
                     nc.tensor.transpose(bank[:, t, :], xm32[:, a, t, :], ident[:])
                 nc.vector.tensor_copy(
@@ -123,11 +125,11 @@ def tile_condtransportkernel_pa_kernel(tc, x_mu, y_mean, y_var, X_mean, Z_mean, 
                 scales=q_scales[:, cols],
                 in_=q_grouped[:].rearrange("q j t -> q (j t)"),
             )
-            yy_rep = work.tile([P, HALF_TILES, P], F32, bufs=1)
+            yy_rep = work.tile([P, HALF_TILES, P], F32)
             nc.vector.tensor_scalar_mul(
                 out=yy_rep[:], in0=yy[:, rows].unsqueeze(2).to_broadcast([P, HALF_TILES, P]), scalar1=0.5
             )
-            bank = psum.tile([P, HALF_TILES, P], F32, tag="flip", bufs=3)
+            bank = psum.tile([P, HALF_TILES, P], F32, tag="bank", bufs=8)
             for a in range(HALF_TILES):
                 nc.tensor.transpose(bank[:, a, :], yy_rep[:, a, :], ident[:])
             nc.vector.tensor_copy(out=yy_rows[:, cols], in_=bank[:].rearrange("p a j -> p (a j)"))
@@ -135,9 +137,9 @@ def tile_condtransportkernel_pa_kernel(tc, x_mu, y_mean, y_var, X_mean, Z_mean, 
         def prepare_points(g):
             x_grouped = work.tile([P, K_PASS * PACK], BF16, align_bytes=64)
             x_words = x_grouped[:].bitcast(F32).rearrange("q (t r u) -> q t r u", t=PACK, u=2)
-            for b in range(2):
+            for b, copy in ((0, nc.scalar.copy), (1, nc.vector.tensor_copy)):
                 blocks = [x_raw[:, g, 2 * b + s, :].bitcast(F32) for s in range(2)]
-                flip_two_blocks(blocks, x_words[:, 2 * b : 2 * b + 2], nc.scalar.copy)
+                flip_two_blocks(blocks, x_words[:, 2 * b : 2 * b + 2], copy)
             cols = slice(g * K_PASS, (g + 1) * K_PASS)
             nc.vector.quantize_mx(out=x_codes[:, cols].bitcast(FP8X4), scales=x_scales[:, cols], in_=x_grouped[:])
             for t in range(PACK):
@@ -161,27 +163,41 @@ def tile_condtransportkernel_pa_kernel(tc, x_mu, y_mean, y_var, X_mean, Z_mean, 
                 in_=z_grouped[:].rearrange("q g c t -> q (g c t)"),
             )
 
-        def lam_row_tile(raw_rows, t, lam_banks):
-            words = raw_rows.bitcast(F32)
-            kinv_grouped = work.tile([P, NX], BF16, bufs=3, align_bytes=64)
-            kinv_words = kinv_grouped[:].bitcast(F32).rearrange("q (g r u) -> q g r u", g=GROUPS, u=2)
-            for b in range(2):
-                blocks = [words[:, (2 * b + c) * 2 * P : (2 * b + c + 1) * 2 * P] for c in range(2)]
-                flip_two_blocks(blocks, kinv_words[:, 2 * b : 2 * b + 2], nc.scalar.copy)
-            kinv_codes = work.tile([P, GROUPS * P], U32, bufs=3, align_bytes=64)
-            kinv_scales = work.tile([P, GROUPS * P], U8, bufs=3, align_bytes=64)
-            nc.vector.quantize_mx(out=kinv_codes[:].bitcast(FP8X4), scales=kinv_scales[:], in_=kinv_grouped[:])
-            for dh in range(2):
-                for g in range(GROUPS):
-                    nc.tensor.matmul_mx(
-                        out=lam_banks[dh][:, t, :],
-                        lhsT=kinv_codes[:, g * P : (g + 1) * P].bitcast(FP8X4),
-                        lhsT_scale=kinv_scales[:, g * P : (g + 1) * P],
-                        rhs=z_codes[:, g, dh * P : (dh + 1) * P].bitcast(FP8X4),
-                        rhs_scale=z_scales[:, g, dh * P : (dh + 1) * P],
-                        start=(g == 0),
-                        stop=(g == GROUPS - 1),
-                    )
+        def flip_kinv(step):
+            grouped = []
+            for s in range(2):
+                words = kinv_raw[step][:, s, :].bitcast(F32)
+                kinv_grouped = work.tile([P, NX], BF16, bufs=4, align_bytes=64)
+                kinv_words = kinv_grouped[:].bitcast(F32).rearrange("q (g r u) -> q g r u", g=GROUPS, u=2)
+                for b in range(2):
+                    blocks = [words[:, (2 * b + c) * 2 * P : (2 * b + c + 1) * 2 * P] for c in range(2)]
+                    flip_two_blocks(blocks, kinv_words[:, 2 * b : 2 * b + 2], nc.scalar.copy)
+                grouped.append(kinv_grouped)
+            return grouped
+
+        def quantise_kinv(grouped):
+            operands = []
+            for kinv_grouped in grouped:
+                kinv_codes = work.tile([P, GROUPS * P], U32, bufs=4, align_bytes=64)
+                kinv_scales = work.tile([P, GROUPS * P], U8, bufs=4, align_bytes=64)
+                nc.vector.quantize_mx(out=kinv_codes[:].bitcast(FP8X4), scales=kinv_scales[:], in_=kinv_grouped[:])
+                operands.append((kinv_codes, kinv_scales))
+            return operands
+
+        def lam_passes(step, operands, lam_banks):
+            for s in range(2):
+                kinv_codes, kinv_scales = operands[s]
+                for dh in range(2):
+                    for g in range(GROUPS):
+                        nc.tensor.matmul_mx(
+                            out=lam_banks[dh][:, 2 * (step % 2) + s, :],
+                            lhsT=kinv_codes[:, g * P : (g + 1) * P].bitcast(FP8X4),
+                            lhsT_scale=kinv_scales[:, g * P : (g + 1) * P],
+                            rhs=z_codes[:, g, dh * P : (dh + 1) * P].bitcast(FP8X4),
+                            rhs_scale=z_scales[:, g, dh * P : (dh + 1) * P],
+                            start=(g == 0),
+                            stop=(g == GROUPS - 1),
+                        )
 
         def quantise_lam(group, lam_banks):
             lam_grouped = work.tile([P, DY, PACK], BF16, align_bytes=64)
@@ -193,13 +209,13 @@ def tile_condtransportkernel_pa_kernel(tc, x_mu, y_mean, y_var, X_mean, Z_mean, 
                 in_=lam_grouped[:].rearrange("p d t -> p (d t)"),
             )
 
-        def k_piece(step):
+        def cross_and_d2(step):
             half, group = divmod(step, GROUPS)
             cols = slice(half * HALF, (half + 1) * HALF)
             minus_half_d2 = work.tile([P, PACK, HALF], F32)
             for t in range(PACK):
                 points = slice((PACK * group + t) * P, (PACK * group + t + 1) * P)
-                cross = psum.tile([P, HALF], F32, tag="cross", bufs=3)
+                cross = psum.tile([P, HALF], F32, tag="bank", bufs=8)
                 nc.tensor.matmul_mx(
                     out=cross[:],
                     lhsT=x_codes[:, points].bitcast(FP8X4),
@@ -217,6 +233,9 @@ def tile_condtransportkernel_pa_kernel(tc, x_mu, y_mean, y_var, X_mean, Z_mean, 
                     op0=ALU.subtract,
                     op1=ALU.subtract,
                 )
+            return minus_half_d2
+
+        def exp_k(minus_half_d2):
             k_grouped = work.tile([P, HALF, PACK], BF16, align_bytes=64)
             for sub in range(2):
                 queries = slice(sub * HALF // 2, (sub + 1) * HALF // 2)
@@ -226,17 +245,25 @@ def tile_condtransportkernel_pa_kernel(tc, x_mu, y_mean, y_var, X_mean, Z_mean, 
                     func=ACT.Exp,
                     scale=1.0 / 64.0,
                 )
+            return k_grouped
+
+        def clamp_and_quantise_k(step, k_grouped):
+            halves = [slice(sub * HALF // 2, (sub + 1) * HALF // 2) for sub in range(2)]
+            for queries in halves:
                 k_flat = k_grouped[:, queries, :].rearrange("p j t -> p (j t)")
                 nc.vector.tensor_scalar_min(out=k_flat, in0=k_flat, scalar1=1.0)
+            for queries in halves:
                 nc.vector.quantize_mx(
-                    out=k_codes[:, step, queries].bitcast(FP8X4), scales=k_scales[:, step, queries], in_=k_flat
+                    out=k_codes[:, step, queries].bitcast(FP8X4),
+                    scales=k_scales[:, step, queries],
+                    in_=k_grouped[:, queries, :].rearrange("p j t -> p (j t)"),
                 )
 
         def out_pair(pair):
             result = work.tile([P, 2, DY], F32)
             for s in range(2):
                 half, col = divmod(2 * pair + s, HALF_TILES)
-                acc = psum.tile([P, DY], F32, tag="cross", bufs=3)
+                acc = psum.tile([P, DY], F32, tag="bank", bufs=8)
                 for g in range(GROUPS):
                     nc.tensor.matmul_mx(
                         out=acc[:],
@@ -254,22 +281,38 @@ def tile_condtransportkernel_pa_kernel(tc, x_mu, y_mean, y_var, X_mean, Z_mean, 
 
         prepare_queries(0)
         prepare_points(0)
+        prepare_queries(1)
+        prepare_points(1)
         prepare_z()
-        for lam_group in range(GROUPS):
-            lam_lo = psum.tile([P, PACK, P], F32)
-            lam_hi = psum.tile([P, PACK, P], F32)
-            for part in range(2):
-                step = 2 * lam_group + part
-                for s in range(2):
-                    lam_row_tile(kinv_raw[step][:, s, :], 2 * part + s, [lam_lo, lam_hi])
-                if step + KINV_AHEAD < STEPS:
-                    load_kinv(step + KINV_AHEAD)
-                if part == 1:
-                    quantise_lam(lam_group, [lam_lo, lam_hi])
-                k_piece(step)
-                if step + 1 < GROUPS:
-                    prepare_points(step + 1)
-                if step == 1:
-                    prepare_queries(1)
-        for pair in range(Q_TILES // 2):
-            out_pair(pair)
+        prepare_points(2)
+        prepare_points(3)
+
+        kinv_mx = {}
+        for step in range(2):
+            kinv_mx[step] = quantise_kinv(flip_kinv(step))
+        minus_half_d2 = cross_and_d2(0)
+        lam_lo = psum.tile([P, PACK, P], F32, tag="bank", bufs=8)
+        lam_hi = psum.tile([P, PACK, P], F32, tag="bank", bufs=8)
+        lam_passes(0, kinv_mx[0], [lam_lo, lam_hi])
+        for step in range(STEPS):
+            k_grouped = exp_k(minus_half_d2)
+            if step + 2 < STEPS:
+                kinv_flipped = flip_kinv(step + 2)
+            if step + KINV_AHEAD < STEPS:
+                kinv_raw[step + KINV_AHEAD] = load_kinv(step + KINV_AHEAD)
+            if step + 1 < STEPS:
+                minus_half_d2 = cross_and_d2(step + 1)
+                if step % 2 == 1:
+                    lam_lo = psum.tile([P, PACK, P], F32, tag="bank", bufs=8)
+                    lam_hi = psum.tile([P, PACK, P], F32, tag="bank", bufs=8)
+                lam_passes(step + 1, kinv_mx[step + 1], [lam_lo, lam_hi])
+            if step == STEPS - 1:
+                out_pair(0)
+                out_pair(1)
+            clamp_and_quantise_k(step, k_grouped)
+            if step + 2 < STEPS:
+                kinv_mx[step + 2] = quantise_kinv(kinv_flipped)
+            if step + 1 < STEPS and step % 2 == 0:
+                quantise_lam(step // 2, [lam_lo, lam_hi])
+        out_pair(2)
+        out_pair(3)

@@ -46,7 +46,7 @@ def tile_condtransportkernel_pa_kernel(tc, x_mu, y_mean, y_var, X_mean, Z_mean, 
         yy_rows = keep.tile([P, NT], F32)
         x_codes = keep.tile([P, NX], U32, align_bytes=64)
         x_scales = keep.tile([P, NX], U8, align_bytes=64)
-        xx = keep.tile([P, GROUPS, PACK], F32)
+        xx = keep.tile([P, GROUPS, 2], F32)
         xx_half = keep.tile([P, GROUPS, PACK], F32)
         z_codes = keep.tile([P, GROUPS, DY], U32, align_bytes=64)
         z_scales = keep.tile([P, GROUPS, DY], U8, align_bytes=64)
@@ -137,17 +137,28 @@ def tile_condtransportkernel_pa_kernel(tc, x_mu, y_mean, y_var, X_mean, Z_mean, 
         def prepare_points(g):
             x_grouped = work.tile([P, K_PASS * PACK], BF16, align_bytes=64)
             x_words = x_grouped[:].bitcast(F32).rearrange("q (t r u) -> q t r u", t=PACK, u=2)
-            for b, copy in ((0, nc.scalar.copy), (1, nc.vector.tensor_copy)):
+            for b in range(2):
                 blocks = [x_raw[:, g, 2 * b + s, :].bitcast(F32) for s in range(2)]
-                flip_two_blocks(blocks, x_words[:, 2 * b : 2 * b + 2], copy)
+                flip_two_blocks(blocks, x_words[:, 2 * b : 2 * b + 2], nc.scalar.copy)
             cols = slice(g * K_PASS, (g + 1) * K_PASS)
             nc.vector.quantize_mx(out=x_codes[:, cols].bitcast(FP8X4), scales=x_scales[:, cols], in_=x_grouped[:])
-            for t in range(PACK):
+            for t in range(2):
                 square = work.tile([P, DM], BF16, tag="square")
                 nc.scalar.activation(
                     out=square[:], in_=x_raw[:, g, t, :], func=ACT.Square, accum_out=xx[:, g, t : t + 1]
                 )
-            nc.vector.tensor_scalar_mul(out=xx_half[:, g, :], in0=xx[:, g, :], scalar1=0.5)
+            for t in range(2, PACK):
+                half_square = work.tile([P, DM], BF16, tag="half_square")
+                nc.vector.scalar_tensor_tensor(
+                    out=half_square[:],
+                    in0=x_raw[:, g, t, :],
+                    scalar=0.5,
+                    in1=x_raw[:, g, t, :],
+                    op0=ALU.mult,
+                    op1=ALU.mult,
+                    accum_out=xx_half[:, g, t : t + 1],
+                )
+            nc.vector.tensor_scalar_mul(out=xx_half[:, g, 0:2], in0=xx[:, g, :], scalar1=0.5)
 
         def prepare_z():
             z_grouped = work.tile([P, GROUPS, DY, PACK], BF16, bufs=1, align_bytes=64)
@@ -201,8 +212,10 @@ def tile_condtransportkernel_pa_kernel(tc, x_mu, y_mean, y_var, X_mean, Z_mean, 
 
         def quantise_lam(group, lam_banks):
             lam_grouped = work.tile([P, DY, PACK], BF16, align_bytes=64)
-            nc.scalar.copy(out=lam_grouped[:, 0:P, :], in_=lam_banks[0][:].rearrange("p t d -> p d t"))
-            nc.vector.tensor_copy(out=lam_grouped[:, P:DY, :], in_=lam_banks[1][:].rearrange("p t d -> p d t"))
+            for dh in range(2):
+                nc.scalar.copy(
+                    out=lam_grouped[:, dh * P : (dh + 1) * P, :], in_=lam_banks[dh][:].rearrange("p t d -> p d t")
+                )
             nc.vector.quantize_mx(
                 out=lam_codes[:, group, :].bitcast(FP8X4),
                 scales=lam_scales[:, group, :],

@@ -46,7 +46,7 @@ def tile_condtransportkernel_pa_kernel(tc, x_mu, y_mean, y_var, X_mean, Z_mean, 
         yy_rows = keep.tile([P, NT], F32)
         x_codes = keep.tile([P, NX], U32, align_bytes=64)
         x_scales = keep.tile([P, NX], U8, align_bytes=64)
-        xx = keep.tile([P, GROUPS, 2], F32)
+        xx = keep.tile([P, GROUPS, 3], F32)
         xx_half = keep.tile([P, GROUPS, PACK], F32)
         z_codes = keep.tile([P, GROUPS, DY], U32, align_bytes=64)
         z_scales = keep.tile([P, GROUPS, DY], U8, align_bytes=64)
@@ -142,12 +142,12 @@ def tile_condtransportkernel_pa_kernel(tc, x_mu, y_mean, y_var, X_mean, Z_mean, 
                 flip_two_blocks(blocks, x_words[:, 2 * b : 2 * b + 2], nc.scalar.copy)
             cols = slice(g * K_PASS, (g + 1) * K_PASS)
             nc.vector.quantize_mx(out=x_codes[:, cols].bitcast(FP8X4), scales=x_scales[:, cols], in_=x_grouped[:])
-            for t in range(2):
+            for t in range(3):
                 square = work.tile([P, DM], BF16, tag="square")
                 nc.scalar.activation(
                     out=square[:], in_=x_raw[:, g, t, :], func=ACT.Square, accum_out=xx[:, g, t : t + 1]
                 )
-            for t in range(2, PACK):
+            for t in range(3, PACK):
                 half_square = work.tile([P, DM], BF16, tag="half_square")
                 nc.vector.scalar_tensor_tensor(
                     out=half_square[:],
@@ -158,7 +158,7 @@ def tile_condtransportkernel_pa_kernel(tc, x_mu, y_mean, y_var, X_mean, Z_mean, 
                     op1=ALU.mult,
                     accum_out=xx_half[:, g, t : t + 1],
                 )
-            nc.vector.tensor_scalar_mul(out=xx_half[:, g, 0:2], in0=xx[:, g, :], scalar1=0.5)
+            nc.vector.tensor_scalar_mul(out=xx_half[:, g, 0:3], in0=xx[:, g, :], scalar1=0.5)
 
         def prepare_z():
             z_grouped = work.tile([P, GROUPS, DY, PACK], BF16, bufs=1, align_bytes=64)

@@ -1,3 +1,4 @@
+import math
 from contextlib import ExitStack
 
 import concourse.mybir as mybir
@@ -22,6 +23,7 @@ Q_TILES = NT // P
 HALF = 512
 HALF_TILES = HALF // P
 STEPS = 2 * GROUPS
+HALF_ROOT = math.sqrt(0.5)
 KINV_AHEAD = 4
 
 FLOPS = 2 * NX * NX * DY + 2 * NX * NT * DM + 2 * NX * NT * DY
@@ -46,7 +48,6 @@ def tile_condtransportkernel_pa_kernel(tc, x_mu, y_mean, y_var, X_mean, Z_mean, 
         yy_rows = keep.tile([P, NT], F32)
         x_codes = keep.tile([P, NX], U32, align_bytes=64)
         x_scales = keep.tile([P, NX], U8, align_bytes=64)
-        xx = keep.tile([P, GROUPS, 3], F32)
         xx_half = keep.tile([P, GROUPS, PACK], F32)
         z_codes = keep.tile([P, GROUPS, DY], U32, align_bytes=64)
         z_scales = keep.tile([P, GROUPS, DY], U8, align_bytes=64)
@@ -145,7 +146,7 @@ def tile_condtransportkernel_pa_kernel(tc, x_mu, y_mean, y_var, X_mean, Z_mean, 
             for t in range(3):
                 square = work.tile([P, DM], BF16, tag="square")
                 nc.scalar.activation(
-                    out=square[:], in_=x_raw[:, g, t, :], func=ACT.Square, accum_out=xx[:, g, t : t + 1]
+                    out=square[:], in_=x_raw[:, g, t, :], func=ACT.Square, scale=HALF_ROOT, accum_out=xx_half[:, g, t : t + 1]
                 )
             for t in range(3, PACK):
                 half_square = work.tile([P, DM], BF16, tag="half_square")
@@ -158,7 +159,6 @@ def tile_condtransportkernel_pa_kernel(tc, x_mu, y_mean, y_var, X_mean, Z_mean, 
                     op1=ALU.mult,
                     accum_out=xx_half[:, g, t : t + 1],
                 )
-            nc.vector.tensor_scalar_mul(out=xx_half[:, g, 0:3], in0=xx[:, g, :], scalar1=0.5)
 
         def prepare_z():
             z_grouped = work.tile([P, GROUPS, DY, PACK], BF16, bufs=1, align_bytes=64)
@@ -273,7 +273,7 @@ def tile_condtransportkernel_pa_kernel(tc, x_mu, y_mean, y_var, X_mean, Z_mean, 
                 )
 
         def out_pair(pair):
-            result = work.tile([P, 2, DY], F32)
+            result = work.tile([P, 2, DY], F32, bufs=4)
             for s in range(2):
                 half, col = divmod(2 * pair + s, HALF_TILES)
                 acc = psum.tile([P, DY], F32, tag="bank", bufs=8)

@@ -44,7 +44,7 @@ def tile_condtransportkernel_pa_kernel(tc, x_mu, y_mean, y_var, X_mean, Z_mean, 
         ident = keep.tile([P, P], F32)
         q_codes = keep.tile([P, NT], U32, align_bytes=64)
         q_scales = keep.tile([P, NT], U8, align_bytes=64)
-        yy = keep.tile([P, Q_TILES], F32)
+        yy = keep.tile([P, Q_TILES, 2], F32)
         yy_rows = keep.tile([P, NT], F32)
         x_codes = keep.tile([P, NX], U32, align_bytes=64)
         x_scales = keep.tile([P, NX], U8, align_bytes=64)
@@ -98,41 +98,36 @@ def tile_condtransportkernel_pa_kernel(tc, x_mu, y_mean, y_var, X_mean, Z_mean, 
         def prepare_queries(half):
             rows = slice(half * HALF_TILES, (half + 1) * HALF_TILES)
             cols = slice(half * HALF, (half + 1) * HALF)
-            xm32 = work.tile([P, HALF_TILES, PACK, P], F32)
-            nc.scalar.copy(out=xm32[:, :, 0:2, :], in_=x_mu_sb[:, rows, :].rearrange("p a (q e) -> p a e q", e=2))
-            nc.vector.tensor_tensor(
-                out=xm32[:, :, 2:4, :],
-                in0=y_mean_sb[:, rows, :].rearrange("p a (q e) -> p a e q", e=2),
-                in1=y_var_sb[:, rows, :].rearrange("p a (q e) -> p a e q", e=2),
-                op=ALU.add,
-            )
-            q_grouped = work.tile([P, HALF, PACK], BF16, align_bytes=64)
+            y_sum = work.tile([P, HALF_TILES, DY], BF16)
+            nc.vector.tensor_tensor(out=y_sum[:], in0=y_mean_sb[:, rows, :], in1=y_var_sb[:, rows, :], op=ALU.add)
+            y_sum32 = work.tile([P, HALF_TILES, DY], F32)
+            nc.vector.tensor_tensor(out=y_sum32[:], in0=y_mean_sb[:, rows, :], in1=y_var_sb[:, rows, :], op=ALU.add)
+            q_grouped = work.tile([P, HALF * PACK], BF16, align_bytes=64)
+            q_words = q_grouped[:].bitcast(F32).rearrange("q (a r u) -> q a r u", a=HALF_TILES, u=2)
+            for b in range(HALF_TILES // 2):
+                bank = psum.tile([P, 2, 2, P], F32, tag="bank", bufs=8)
+                for s in range(2):
+                    a = 2 * b + s
+                    nc.tensor.transpose(bank[:, s, 0, :], x_mu_sb[:, half * HALF_TILES + a, :].bitcast(F32), ident[:])
+                    nc.tensor.transpose(bank[:, s, 1, :], y_sum[:, a, :].bitcast(F32), ident[:])
+                nc.vector.tensor_copy(out=q_words[:, 2 * b : 2 * b + 2], in_=bank[:].rearrange("q a u r -> q a r u"))
+            nc.vector.quantize_mx(out=q_codes[:, cols].bitcast(FP8X4), scales=q_scales[:, cols], in_=q_grouped[:])
             for a in range(HALF_TILES):
-                square = work.tile([P, DM], BF16, tag="square")
-                nc.scalar.activation(
-                    out=square[:],
-                    in_=xm32[:, a].rearrange("p t q -> p (t q)"),
-                    func=ACT.Square,
-                    accum_out=yy[:, half * HALF_TILES + a : half * HALF_TILES + a + 1],
-                )
-                bank = psum.tile([P, PACK, P], F32, tag="bank", bufs=8)
-                for t in range(PACK):
-                    nc.tensor.transpose(bank[:, t, :], xm32[:, a, t, :], ident[:])
-                nc.vector.tensor_copy(
-                    out=q_grouped[:, a * P : (a + 1) * P, :], in_=bank[:].rearrange("q t j -> q j t")
-                )
-            nc.vector.quantize_mx(
-                out=q_codes[:, cols].bitcast(FP8X4),
-                scales=q_scales[:, cols],
-                in_=q_grouped[:].rearrange("q j t -> q (j t)"),
-            )
-            yy_rep = work.tile([P, HALF_TILES, P], F32)
-            nc.vector.tensor_scalar_mul(
-                out=yy_rep[:], in0=yy[:, rows].unsqueeze(2).to_broadcast([P, HALF_TILES, P]), scalar1=0.5
-            )
+                tile_a = half * HALF_TILES + a
+                for part, values in enumerate((x_mu_sb[:, tile_a, :], y_sum32[:, a, :])):
+                    square = work.tile([P, DX], BF16, tag="q_square")
+                    nc.scalar.activation(
+                        out=square[:],
+                        in_=values,
+                        func=ACT.Square,
+                        scale=HALF_ROOT,
+                        accum_out=yy[:, tile_a, part : part + 1],
+                    )
+            yy_sum = work.tile([P, HALF_TILES], F32)
+            nc.vector.tensor_tensor(out=yy_sum[:], in0=yy[:, rows, 0], in1=yy[:, rows, 1], op=ALU.add)
             bank = psum.tile([P, HALF_TILES, P], F32, tag="bank", bufs=8)
             for a in range(HALF_TILES):
-                nc.tensor.transpose(bank[:, a, :], yy_rep[:, a, :], ident[:])
+                nc.tensor.transpose(bank[:, a, :], yy_sum[:, a : a + 1].to_broadcast([P, P]), ident[:])
             nc.vector.tensor_copy(out=yy_rows[:, cols], in_=bank[:].rearrange("p a j -> p (a j)"))
 
         def prepare_points(g):

@@ -56,8 +56,8 @@ def tile_condtransportkernel_pa_kernel(tc, x_mu, y_mean, y_var, X_mean, Z_mean, 
         k_codes = keep.tile([P, STEPS, HALF], U32, align_bytes=64)
         k_scales = keep.tile([P, STEPS, HALF], U8, align_bytes=64)
 
-        def load_queries(half):
-            rows = slice(half * HALF_TILES, (half + 1) * HALF_TILES)
+        def load_queries(first, count):
+            rows = slice(first, first + count)
             for sb, dram in ((x_mu_sb, x_mu), (y_mean_sb, y_mean), (y_var_sb, y_var)):
                 nc.sync.dma_start(out=sb[:, rows, :], in_=dram.rearrange("(p a) c -> p a c", a=Q_TILES)[:, rows, :])
 
@@ -70,15 +70,17 @@ def tile_condtransportkernel_pa_kernel(tc, x_mu, y_mean, y_var, X_mean, Z_mean, 
             nc.sync.dma_start(out=raw[:], in_=view[step // 2, step % 2])
             return raw
 
-        load_queries(0)
+        kinv_raw = {}
+        load_queries(0, 2)
+        load_queries(2, 2)
         load_points(0)
-        load_queries(1)
+        load_queries(HALF_TILES, HALF_TILES)
         load_points(1)
-        nc.sync.dma_start(out=z_raw[:], in_=Z_mean.rearrange("(s q e) c -> q s e c", q=P, e=2))
-        kinv_raw = {0: load_kinv(0)}
         load_points(2)
-        kinv_raw[1] = load_kinv(1)
         load_points(3)
+        nc.sync.dma_start(out=z_raw[:], in_=Z_mean.rearrange("(s q e) c -> q s e c", q=P, e=2))
+        kinv_raw[0] = load_kinv(0)
+        kinv_raw[1] = load_kinv(1)
         kinv_raw[2] = load_kinv(2)
         kinv_raw[3] = load_kinv(3)
 
@@ -99,9 +101,17 @@ def tile_condtransportkernel_pa_kernel(tc, x_mu, y_mean, y_var, X_mean, Z_mean, 
             rows = slice(half * HALF_TILES, (half + 1) * HALF_TILES)
             cols = slice(half * HALF, (half + 1) * HALF)
             y_sum = work.tile([P, HALF_TILES, DY], BF16)
-            nc.vector.tensor_tensor(out=y_sum[:], in0=y_mean_sb[:, rows, :], in1=y_var_sb[:, rows, :], op=ALU.add)
+            for b in range(HALF_TILES // 2):
+                pair = slice(half * HALF_TILES + 2 * b, half * HALF_TILES + 2 * b + 2)
+                nc.vector.tensor_tensor(
+                    out=y_sum[:, 2 * b : 2 * b + 2, :], in0=y_mean_sb[:, pair, :], in1=y_var_sb[:, pair, :], op=ALU.add
+                )
             y_sum32 = work.tile([P, HALF_TILES, DY], F32)
-            nc.vector.tensor_tensor(out=y_sum32[:], in0=y_mean_sb[:, rows, :], in1=y_var_sb[:, rows, :], op=ALU.add)
+            for b in range(HALF_TILES // 2):
+                pair = slice(half * HALF_TILES + 2 * b, half * HALF_TILES + 2 * b + 2)
+                nc.vector.tensor_tensor(
+                    out=y_sum32[:, 2 * b : 2 * b + 2, :], in0=y_mean_sb[:, pair, :], in1=y_var_sb[:, pair, :], op=ALU.add
+                )
             q_grouped = work.tile([P, HALF * PACK], BF16, align_bytes=64)
             q_words = q_grouped[:].bitcast(F32).rearrange("q (a r u) -> q a r u", a=HALF_TILES, u=2)
             for b in range(HALF_TILES // 2):
@@ -138,12 +148,12 @@ def tile_condtransportkernel_pa_kernel(tc, x_mu, y_mean, y_var, X_mean, Z_mean, 
                 flip_two_blocks(blocks, x_words[:, 2 * b : 2 * b + 2], nc.scalar.copy)
             cols = slice(g * K_PASS, (g + 1) * K_PASS)
             nc.vector.quantize_mx(out=x_codes[:, cols].bitcast(FP8X4), scales=x_scales[:, cols], in_=x_grouped[:])
-            for t in range(3):
+            for t in range(2 if g < 1 else 3):
                 square = work.tile([P, DM], BF16, tag="square")
                 nc.scalar.activation(
                     out=square[:], in_=x_raw[:, g, t, :], func=ACT.Square, scale=HALF_ROOT, accum_out=xx_half[:, g, t : t + 1]
                 )
-            for t in range(3, PACK):
+            for t in range(2 if g < 1 else 3, PACK):
                 half_square = work.tile([P, DM], BF16, tag="half_square")
                 nc.vector.scalar_tensor_tensor(
                     out=half_square[:],
@@ -291,9 +301,9 @@ def tile_condtransportkernel_pa_kernel(tc, x_mu, y_mean, y_var, X_mean, Z_mean, 
         prepare_points(0)
         prepare_queries(1)
         prepare_points(1)
-        prepare_z()
         prepare_points(2)
         prepare_points(3)
+        prepare_z()
 
         kinv_mx = {}
         for step in range(2):

@@ -101,17 +101,13 @@ def tile_condtransportkernel_pa_kernel(tc, x_mu, y_mean, y_var, X_mean, Z_mean, 
             rows = slice(half * HALF_TILES, (half + 1) * HALF_TILES)
             cols = slice(half * HALF, (half + 1) * HALF)
             y_sum = work.tile([P, HALF_TILES, DY], BF16)
-            for b in range(HALF_TILES // 2):
-                pair = slice(half * HALF_TILES + 2 * b, half * HALF_TILES + 2 * b + 2)
-                nc.vector.tensor_tensor(
-                    out=y_sum[:, 2 * b : 2 * b + 2, :], in0=y_mean_sb[:, pair, :], in1=y_var_sb[:, pair, :], op=ALU.add
-                )
             y_sum32 = work.tile([P, HALF_TILES, DY], F32)
             for b in range(HALF_TILES // 2):
                 pair = slice(half * HALF_TILES + 2 * b, half * HALF_TILES + 2 * b + 2)
-                nc.vector.tensor_tensor(
-                    out=y_sum32[:, 2 * b : 2 * b + 2, :], in0=y_mean_sb[:, pair, :], in1=y_var_sb[:, pair, :], op=ALU.add
-                )
+                for total in (y_sum32, y_sum):
+                    nc.vector.tensor_tensor(
+                        out=total[:, 2 * b : 2 * b + 2, :], in0=y_mean_sb[:, pair, :], in1=y_var_sb[:, pair, :], op=ALU.add
+                    )
             q_grouped = work.tile([P, HALF * PACK], BF16, align_bytes=64)
             q_words = q_grouped[:].bitcast(F32).rearrange("q (a r u) -> q a r u", a=HALF_TILES, u=2)
             for b in range(HALF_TILES // 2):
@@ -253,10 +249,9 @@ def tile_condtransportkernel_pa_kernel(tc, x_mu, y_mean, y_var, X_mean, Z_mean, 
                 )
             return minus_half_d2
 
-        def exp_k(minus_half_d2):
+        def exp_k(minus_half_d2, parts):
             k_grouped = work.tile([P, HALF, PACK], BF16, align_bytes=64)
-            for sub in range(2):
-                queries = slice(sub * HALF // 2, (sub + 1) * HALF // 2)
+            for queries in parts:
                 nc.scalar.activation(
                     out=k_grouped[:, queries, :].rearrange("p (c i) t -> p c t i", i=4),
                     in_=minus_half_d2[:, :, queries].rearrange("p t (c i) -> p c t i", i=4),
@@ -265,22 +260,21 @@ def tile_condtransportkernel_pa_kernel(tc, x_mu, y_mean, y_var, X_mean, Z_mean, 
                 )
             return k_grouped
 
-        def clamp_and_quantise_k(step, k_grouped):
-            halves = [slice(sub * HALF // 2, (sub + 1) * HALF // 2) for sub in range(2)]
-            for queries in halves:
+        def clamp_and_quantise_k(step, k_grouped, parts):
+            for queries in parts:
                 k_flat = k_grouped[:, queries, :].rearrange("p j t -> p (j t)")
                 nc.vector.tensor_scalar_min(out=k_flat, in0=k_flat, scalar1=1.0)
-            for queries in halves:
+            for queries in parts:
                 nc.vector.quantize_mx(
                     out=k_codes[:, step, queries].bitcast(FP8X4),
                     scales=k_scales[:, step, queries],
                     in_=k_grouped[:, queries, :].rearrange("p j t -> p (j t)"),
                 )
 
-        def out_pair(pair):
-            result = work.tile([P, 2, DY], F32, bufs=4)
-            for s in range(2):
-                half, col = divmod(2 * pair + s, HALF_TILES)
+        def out_tiles(first, count):
+            result = work.tile([P, count, DY], F32, tag=f"result_{count}", bufs=4, name="result")
+            for s in range(count):
+                half, col = divmod(first + s, HALF_TILES)
                 acc = psum.tile([P, DY], F32, tag="bank", bufs=8)
                 for g in range(GROUPS):
                     nc.tensor.matmul_mx(
@@ -292,9 +286,9 @@ def tile_condtransportkernel_pa_kernel(tc, x_mu, y_mean, y_var, X_mean, Z_mean, 
                         start=(g == 0),
                         stop=(g == GROUPS - 1),
                     )
-                nc.vector.tensor_tensor(out=result[:, s, :], in0=acc[:], in1=y_mean_sb[:, 2 * pair + s, :], op=ALU.add)
+                nc.vector.tensor_tensor(out=result[:, s, :], in0=acc[:], in1=y_mean_sb[:, first + s, :], op=ALU.add)
             nc.sync.dma_start(
-                out=out.rearrange("(p a) d -> p a d", a=Q_TILES)[:, 2 * pair : 2 * pair + 2, :], in_=result[:]
+                out=out.rearrange("(p a) d -> p a d", a=Q_TILES)[:, first : first + count, :], in_=result[:]
             )
 
         prepare_queries(0)
@@ -305,6 +299,8 @@ def tile_condtransportkernel_pa_kernel(tc, x_mu, y_mean, y_var, X_mean, Z_mean, 
         prepare_points(3)
         prepare_z()
 
+        halves = [slice(0, HALF // 2), slice(HALF // 2, HALF)]
+        last_parts = [slice(i * P, (i + 1) * P) for i in range(HALF_TILES)]
         kinv_mx = {}
         for step in range(2):
             kinv_mx[step] = quantise_kinv(flip_kinv(step))
@@ -313,7 +309,8 @@ def tile_condtransportkernel_pa_kernel(tc, x_mu, y_mean, y_var, X_mean, Z_mean, 
         lam_hi = psum.tile([P, PACK, P], F32, tag="bank", bufs=8)
         lam_passes(0, kinv_mx[0], [lam_lo, lam_hi])
         for step in range(STEPS):
-            k_grouped = exp_k(minus_half_d2)
+            parts = last_parts if step == STEPS - 1 else halves
+            k_grouped = exp_k(minus_half_d2, parts)
             if step + 2 < STEPS:
                 kinv_flipped = flip_kinv(step + 2)
             if step + KINV_AHEAD < STEPS:
@@ -325,12 +322,14 @@ def tile_condtransportkernel_pa_kernel(tc, x_mu, y_mean, y_var, X_mean, Z_mean, 
                     lam_hi = psum.tile([P, PACK, P], F32, tag="bank", bufs=8)
                 lam_passes(step + 1, kinv_mx[step + 1], [lam_lo, lam_hi])
             if step == STEPS - 1:
-                out_pair(0)
-                out_pair(1)
-            clamp_and_quantise_k(step, k_grouped)
+                out_tiles(0, 2)
+                out_tiles(2, 2)
+            clamp_and_quantise_k(step, k_grouped, parts)
             if step + 2 < STEPS:
                 kinv_mx[step + 2] = quantise_kinv(kinv_flipped)
             if step + 1 < STEPS and step % 2 == 0:
                 quantise_lam(step // 2, [lam_lo, lam_hi])
-        out_pair(2)
-        out_pair(3)
+        out_tiles(4, 1)
+        out_tiles(5, 1)
+        out_tiles(6, 1)
+        out_tiles(7, 1)

@@ -307,7 +307,6 @@ def tile_condtransportkernel_pa_kernel(tc, x_mu, y_mean, y_var, X_mean, Z_mean, 
         minus_half_d2 = cross_and_d2(0)
         lam_lo = psum.tile([P, PACK, P], F32, tag="bank", bufs=8)
         lam_hi = psum.tile([P, PACK, P], F32, tag="bank", bufs=8)
-        lam_passes(0, kinv_mx[0], [lam_lo, lam_hi])
         for step in range(STEPS):
             parts = last_parts if step == STEPS - 1 else halves
             k_grouped = exp_k(minus_half_d2, parts)
@@ -320,6 +319,8 @@ def tile_condtransportkernel_pa_kernel(tc, x_mu, y_mean, y_var, X_mean, Z_mean, 
                 if step % 2 == 1:
                     lam_lo = psum.tile([P, PACK, P], F32, tag="bank", bufs=8)
                     lam_hi = psum.tile([P, PACK, P], F32, tag="bank", bufs=8)
+                if step == 0:
+                    lam_passes(0, kinv_mx[0], [lam_lo, lam_hi])
                 lam_passes(step + 1, kinv_mx[step + 1], [lam_lo, lam_hi])
             if step == STEPS - 1:
                 out_tiles(0, 2)

import math
from contextlib import ExitStack

import concourse.mybir as mybir
from concourse.masks import make_identity

F32 = mybir.dt.float32
BF16 = mybir.dt.bfloat16
U32 = mybir.dt.uint32
U8 = mybir.dt.uint8
FP8X4 = mybir.dt.float8_e4m3fn_x4
ALU = mybir.AluOpType
ACT = mybir.ActivationFunctionType

P = 128
PACK = 4
K_PASS = P * PACK

NX, NT, DX, DY = 2048, 1024, 256, 256
DM = DX + DY
GROUPS = NX // K_PASS
Q_TILES = NT // P
HALF = 512
HALF_TILES = HALF // P
STEPS = 2 * GROUPS
HALF_ROOT = math.sqrt(0.5)
KINV_AHEAD = 4

FLOPS = 2 * NX * NX * DY + 2 * NX * NT * DM + 2 * NX * NT * DY


def tile_condtransportkernel_pa_kernel(tc, x_mu, y_mean, y_var, X_mean, Z_mean, kXXmean_inv, out):
    nc = tc.nc
    with ExitStack() as ctx:
        keep = ctx.enter_context(tc.tile_pool(name="keep", bufs=1))
        work = ctx.enter_context(tc.tile_pool(name="work", bufs=2))
        psum = ctx.enter_context(tc.psum_pool(name="psum", bufs=1))

        x_mu_sb = keep.tile([P, Q_TILES, DX], BF16)
        y_mean_sb = keep.tile([P, Q_TILES, DY], BF16)
        y_var_sb = keep.tile([P, Q_TILES, DY], BF16)
        x_raw = keep.tile([P, GROUPS, PACK, DM], BF16)
        z_raw = keep.tile([P, 2 * GROUPS, 2, DY], BF16)
        ident = keep.tile([P, P], F32)
        q_codes = keep.tile([P, NT], U32, align_bytes=64)
        q_scales = keep.tile([P, NT], U8, align_bytes=64)
        yy = keep.tile([P, Q_TILES, 2], F32)
        yy_rows = keep.tile([P, NT], F32)
        x_codes = keep.tile([P, NX], U32, align_bytes=64)
        x_scales = keep.tile([P, NX], U8, align_bytes=64)
        xx_half = keep.tile([P, GROUPS, PACK], F32)
        z_codes = keep.tile([P, GROUPS, DY], U32, align_bytes=64)
        z_scales = keep.tile([P, GROUPS, DY], U8, align_bytes=64)
        lam_codes = keep.tile([P, GROUPS, DY], U32, align_bytes=64)
        lam_scales = keep.tile([P, GROUPS, DY], U8, align_bytes=64)
        k_codes = keep.tile([P, STEPS, HALF], U32, align_bytes=64)
        k_scales = keep.tile([P, STEPS, HALF], U8, align_bytes=64)

        def load_queries(first, count):
            rows = slice(first, first + count)
            for sb, dram in ((x_mu_sb, x_mu), (y_mean_sb, y_mean), (y_var_sb, y_var)):
                nc.sync.dma_start(out=sb[:, rows, :], in_=dram.rearrange("(p a) c -> p a c", a=Q_TILES)[:, rows, :])

        def load_points(g):
            nc.sync.dma_start(out=x_raw[:, g], in_=X_mean.rearrange("(g p t) c -> g p t c", g=GROUPS, t=PACK)[g])

        def load_kinv(step):
            raw = work.tile([P, 2, NX], BF16, tag="kinv_raw", bufs=KINV_AHEAD, name="kinv_raw")
            view = kXXmean_inv.rearrange("(g p h s) m -> g h p s m", g=GROUPS, h=2, s=2)
            nc.sync.dma_start(out=raw[:], in_=view[step // 2, step % 2])
            return raw

        kinv_raw = {}
        load_queries(0, 2)
        load_queries(2, 2)
        load_points(0)
        load_queries(HALF_TILES, HALF_TILES)
        load_points(1)
        load_points(2)
        load_points(3)
        nc.sync.dma_start(out=z_raw[:], in_=Z_mean.rearrange("(s q e) c -> q s e c", q=P, e=2))
        kinv_raw[0] = load_kinv(0)
        kinv_raw[1] = load_kinv(1)
        kinv_raw[2] = load_kinv(2)
        kinv_raw[3] = load_kinv(3)

        make_identity(nc, ident[:])
        zero = keep.tile([P, 1], F32)
        one = keep.tile([P, 1], F32)
        nc.vector.memset(zero[:], 0.0)
        nc.scalar.activation(out=one[:], in_=zero[:], func=ACT.Exp)

        def flip_two_blocks(blocks, grouped_words, copy):
            bank = psum.tile([P, 2, 2, P], F32, tag="bank", bufs=8)
            for b in range(2):
                for u in range(2):
                    nc.tensor.transpose(bank[:, b, u, :], blocks[b][:, u * P : (u + 1) * P], ident[:])
            copy(out=grouped_words, in_=bank[:].rearrange("q b u r -> q b r u"))

        def prepare_queries(half):
            rows = slice(half * HALF_TILES, (half + 1) * HALF_TILES)
            cols = slice(half * HALF, (half + 1) * HALF)
            y_sum = work.tile([P, HALF_TILES, DY], BF16)
            y_sum32 = work.tile([P, HALF_TILES, DY], F32)
            for b in range(HALF_TILES // 2):
                pair = slice(half * HALF_TILES + 2 * b, half * HALF_TILES + 2 * b + 2)
                for total in (y_sum32, y_sum):
                    nc.vector.tensor_tensor(
                        out=total[:, 2 * b : 2 * b + 2, :], in0=y_mean_sb[:, pair, :], in1=y_var_sb[:, pair, :], op=ALU.add
                    )
            q_grouped = work.tile([P, HALF * PACK], BF16, align_bytes=64)
            q_words = q_grouped[:].bitcast(F32).rearrange("q (a r u) -> q a r u", a=HALF_TILES, u=2)
            for b in range(HALF_TILES // 2):
                bank = psum.tile([P, 2, 2, P], F32, tag="bank", bufs=8)
                for s in range(2):
                    a = 2 * b + s
                    nc.tensor.transpose(bank[:, s, 0, :], x_mu_sb[:, half * HALF_TILES + a, :].bitcast(F32), ident[:])
                    nc.tensor.transpose(bank[:, s, 1, :], y_sum[:, a, :].bitcast(F32), ident[:])
                nc.vector.tensor_copy(out=q_words[:, 2 * b : 2 * b + 2], in_=bank[:].rearrange("q a u r -> q a r u"))
            nc.vector.quantize_mx(out=q_codes[:, cols].bitcast(FP8X4), scales=q_scales[:, cols], in_=q_grouped[:])
            for a in range(HALF_TILES):
                tile_a = half * HALF_TILES + a
                for part, values in enumerate((x_mu_sb[:, tile_a, :], y_sum32[:, a, :])):
                    square = work.tile([P, DX], BF16, tag="q_square")
                    nc.scalar.activation(
                        out=square[:],
                        in_=values,
                        func=ACT.Square,
                        scale=HALF_ROOT,
                        accum_out=yy[:, tile_a, part : part + 1],
                    )
            yy_sum = work.tile([P, HALF_TILES], F32)
            nc.vector.tensor_tensor(out=yy_sum[:], in0=yy[:, rows, 0], in1=yy[:, rows, 1], op=ALU.add)
            bank = psum.tile([P, HALF_TILES, P], F32, tag="bank", bufs=8)
            for a in range(HALF_TILES):
                nc.tensor.transpose(bank[:, a, :], yy_sum[:, a : a + 1].to_broadcast([P, P]), ident[:])
            nc.vector.tensor_copy(out=yy_rows[:, cols], in_=bank[:].rearrange("p a j -> p (a j)"))

        def prepare_points(g):
            x_grouped = work.tile([P, K_PASS * PACK], BF16, align_bytes=64)
            x_words = x_grouped[:].bitcast(F32).rearrange("q (t r u) -> q t r u", t=PACK, u=2)
            for b in range(2):
                blocks = [x_raw[:, g, 2 * b + s, :].bitcast(F32) for s in range(2)]
                flip_two_blocks(blocks, x_words[:, 2 * b : 2 * b + 2], nc.scalar.copy)
            cols = slice(g * K_PASS, (g + 1) * K_PASS)
            nc.vector.quantize_mx(out=x_codes[:, cols].bitcast(FP8X4), scales=x_scales[:, cols], in_=x_grouped[:])
            for t in range(2 if g < 1 else 3):
                square = work.tile([P, DM], BF16, tag="square")
                nc.scalar.activation(
                    out=square[:], in_=x_raw[:, g, t, :], func=ACT.Square, scale=HALF_ROOT, accum_out=xx_half[:, g, t : t + 1]
                )
            for t in range(2 if g < 1 else 3, PACK):
                half_square = work.tile([P, DM], BF16, tag="half_square")
                nc.vector.scalar_tensor_tensor(
                    out=half_square[:],
                    in0=x_raw[:, g, t, :],
                    scalar=0.5,
                    in1=x_raw[:, g, t, :],
                    op0=ALU.mult,
                    op1=ALU.mult,
                    accum_out=xx_half[:, g, t : t + 1],
                )

        def prepare_z():
            z_grouped = work.tile([P, GROUPS, DY, PACK], BF16, bufs=1, align_bytes=64)
            z_rows = z_raw[:].rearrange("q (g u) e c -> q g (u e) c", u=2)
            for g in range(GROUPS):
                nc.vector.tensor_copy(
                    out=z_grouped[:, g].rearrange("q (c i) t -> q c t i", i=4),
                    in_=z_rows[:, g].rearrange("q t (c i) -> q c t i", i=4),
                )
            nc.vector.quantize_mx(
                out=z_codes[:].rearrange("q g c -> q (g c)").bitcast(FP8X4),
                scales=z_scales[:].rearrange("q g c -> q (g c)"),
                in_=z_grouped[:].rearrange("q g c t -> q (g c t)"),
            )

        def flip_kinv(step):
            grouped = []
            for s in range(2):
                words = kinv_raw[step][:, s, :].bitcast(F32)
                kinv_grouped = work.tile([P, NX], BF16, bufs=4, align_bytes=64)
                kinv_words = kinv_grouped[:].bitcast(F32).rearrange("q (g r u) -> q g r u", g=GROUPS, u=2)
                for b in range(2):
                    blocks = [words[:, (2 * b + c) * 2 * P : (2 * b + c + 1) * 2 * P] for c in range(2)]
                    flip_two_blocks(blocks, kinv_words[:, 2 * b : 2 * b + 2], nc.scalar.copy)
                grouped.append(kinv_grouped)
            return grouped

        def quantise_kinv(grouped):
            operands = []
            for kinv_grouped in grouped:
                kinv_codes = work.tile([P, GROUPS * P], U32, bufs=4, align_bytes=64)
                kinv_scales = work.tile([P, GROUPS * P], U8, bufs=4, align_bytes=64)
                nc.vector.quantize_mx(out=kinv_codes[:].bitcast(FP8X4), scales=kinv_scales[:], in_=kinv_grouped[:])
                operands.append((kinv_codes, kinv_scales))
            return operands

        def lam_passes(step, operands, lam_banks):
            for s in range(2):
                kinv_codes, kinv_scales = operands[s]
                for dh in range(2):
                    for g in range(GROUPS):
                        nc.tensor.matmul_mx(
                            out=lam_banks[dh][:, 2 * (step % 2) + s, :],
                            lhsT=kinv_codes[:, g * P : (g + 1) * P].bitcast(FP8X4),
                            lhsT_scale=kinv_scales[:, g * P : (g + 1) * P],
                            rhs=z_codes[:, g, dh * P : (dh + 1) * P].bitcast(FP8X4),
                            rhs_scale=z_scales[:, g, dh * P : (dh + 1) * P],
                            start=(g == 0),
                            stop=(g == GROUPS - 1),
                        )

        def quantise_lam(group, lam_banks):
            lam_grouped = work.tile([P, DY, PACK], BF16, align_bytes=64)
            for dh in range(2):
                nc.scalar.copy(
                    out=lam_grouped[:, dh * P : (dh + 1) * P, :], in_=lam_banks[dh][:].rearrange("p t d -> p d t")
                )
            nc.vector.quantize_mx(
                out=lam_codes[:, group, :].bitcast(FP8X4),
                scales=lam_scales[:, group, :],
                in_=lam_grouped[:].rearrange("p d t -> p (d t)"),
            )

        def cross_and_d2(step):
            half, group = divmod(step, GROUPS)
            cols = slice(half * HALF, (half + 1) * HALF)
            minus_half_d2 = work.tile([P, PACK, HALF], F32)
            for t in range(PACK):
                points = slice((PACK * group + t) * P, (PACK * group + t + 1) * P)
                cross = psum.tile([P, HALF], F32, tag="bank", bufs=8)
                nc.tensor.matmul_mx(
                    out=cross[:],
                    lhsT=x_codes[:, points].bitcast(FP8X4),
                    lhsT_scale=x_scales[:, points],
                    rhs=q_codes[:, cols].bitcast(FP8X4),
                    rhs_scale=q_scales[:, cols],
                    start=True,
                    stop=True,
                )
                nc.vector.scalar_tensor_tensor(
                    out=minus_half_d2[:, t, :],
                    in0=cross[:],
                    scalar=xx_half[:, group, t : t + 1],
                    in1=yy_rows[:, cols],
                    op0=ALU.subtract,
                    op1=ALU.subtract,
                )
            return minus_half_d2

        def exp_k(minus_half_d2, parts):
            k_grouped = work.tile([P, HALF, PACK], BF16, align_bytes=64)
            for queries in parts:
                nc.scalar.activation(
                    out=k_grouped[:, queries, :].rearrange("p (c i) t -> p c t i", i=4),
                    in_=minus_half_d2[:, :, queries].rearrange("p t (c i) -> p c t i", i=4),
                    func=ACT.Exp,
                    scale=1.0 / 64.0,
                )
            return k_grouped

        def clamp_and_quantise_k(step, k_grouped, parts):
            for queries in parts:
                k_flat = k_grouped[:, queries, :].rearrange("p j t -> p (j t)")
                nc.vector.tensor_scalar_min(out=k_flat, in0=k_flat, scalar1=1.0)
            for queries in parts:
                nc.vector.quantize_mx(
                    out=k_codes[:, step, queries].bitcast(FP8X4),
                    scales=k_scales[:, step, queries],
                    in_=k_grouped[:, queries, :].rearrange("p j t -> p (j t)"),
                )

        def out_tiles(first, count):
            result = work.tile([P, count, DY], F32, tag=f"result_{count}", bufs=4, name="result")
            for s in range(count):
                half, col = divmod(first + s, HALF_TILES)
                acc = psum.tile([P, DY], F32, tag="bank", bufs=8)
                for g in range(GROUPS):
                    nc.tensor.matmul_mx(
                        out=acc[:],
                        lhsT=k_codes[:, GROUPS * half + g, col * P : (col + 1) * P].bitcast(FP8X4),
                        lhsT_scale=k_scales[:, GROUPS * half + g, col * P : (col + 1) * P],
                        rhs=lam_codes[:, g, :].bitcast(FP8X4),
                        rhs_scale=lam_scales[:, g, :],
                        start=(g == 0),
                        stop=(g == GROUPS - 1),
                    )
                nc.vector.tensor_tensor(out=result[:, s, :], in0=acc[:], in1=y_mean_sb[:, first + s, :], op=ALU.add)
            nc.sync.dma_start(
                out=out.rearrange("(p a) d -> p a d", a=Q_TILES)[:, first : first + count, :], in_=result[:]
            )

        prepare_queries(0)
        prepare_points(0)
        prepare_queries(1)
        prepare_points(1)
        prepare_points(2)
        prepare_points(3)
        prepare_z()

        halves = [slice(0, HALF // 2), slice(HALF // 2, HALF)]
        last_parts = [slice(i * P, (i + 1) * P) for i in range(HALF_TILES)]
        kinv_mx = {}
        for step in range(2):
            kinv_mx[step] = quantise_kinv(flip_kinv(step))
        minus_half_d2 = cross_and_d2(0)
        lam_lo = psum.tile([P, PACK, P], F32, tag="bank", bufs=8)
        lam_hi = psum.tile([P, PACK, P], F32, tag="bank", bufs=8)
        for step in range(STEPS):
            parts = last_parts if step == STEPS - 1 else halves
            k_grouped = exp_k(minus_half_d2, parts)
            if step + 2 < STEPS:
                kinv_flipped = flip_kinv(step + 2)
            if step + KINV_AHEAD < STEPS:
                kinv_raw[step + KINV_AHEAD] = load_kinv(step + KINV_AHEAD)
            if step + 1 < STEPS:
                minus_half_d2 = cross_and_d2(step + 1)
                if step % 2 == 1:
                    lam_lo = psum.tile([P, PACK, P], F32, tag="bank", bufs=8)
                    lam_hi = psum.tile([P, PACK, P], F32, tag="bank", bufs=8)
                if step == 0:
                    lam_passes(0, kinv_mx[0], [lam_lo, lam_hi])
                lam_passes(step + 1, kinv_mx[step + 1], [lam_lo, lam_hi])
            if step == STEPS - 1:
                out_tiles(0, 2)
                out_tiles(2, 2)
            clamp_and_quantise_k(step, k_grouped, parts)
            if step + 2 < STEPS:
                kinv_mx[step + 2] = quantise_kinv(kinv_flipped)
            if step + 1 < STEPS and step % 2 == 0:
                quantise_lam(step // 2, [lam_lo, lam_hi])
        out_tiles(4, 1)
        out_tiles(5, 1)
        out_tiles(6, 1)
        out_tiles(7, 1)
